import numpy as np
import ml_dtypes


def mxq(x, axis, fmt="e4m3"):
    dtype, down = {"e4m3": (ml_dtypes.float8_e4m3fn, 7), "e5m2": (ml_dtypes.float8_e5m2, 14)}[fmt]
    v = np.moveaxis(np.asarray(x, np.float32).astype(ml_dtypes.bfloat16).astype(np.float64), axis, -1)
    blocks = v.reshape(v.shape[:-1] + (-1, 32))
    amax = np.abs(blocks).max(-1, keepdims=True)
    byte = np.maximum(np.where(amax > 0, np.frexp(amax)[1] - 1 + 127, 0) - down, 1)
    scale = np.exp2(byte - 127.0)
    codes = (blocks / scale).astype(np.float32).astype(dtype).astype(np.float64)
    return np.moveaxis((codes * scale).reshape(v.shape), -1, axis)


WIDE = False


def mx_kscale(k):
    if not WIDE:
        return np.ones(k)
    levels = np.array([10, -10, 5, -5, 0])
    a = np.random.permutation(np.resize(levels, k // 512 * 4)).reshape(k // 512, 4)
    idx = np.arange(k)
    return np.exp2(a[idx // 512, idx % 128 // 32])


BF16 = ml_dtypes.bfloat16


def bf(x):
    return np.asarray(x, np.float32).astype(BF16)


def f64(x):
    return np.asarray(x).astype(np.float64)


B, C, H, W, L = 1, 512, 32, 32, 6
N = H * W
EPS = 1e-5
QS = (24.0 / C) ** 0.25
VS = 0.75


def relu_draw():
    return np.maximum(np.random.standard_normal((B, C, H, W)), 0.0)


def setup_inputs():
    t = mx_kscale(C)
    return {"q": bf(relu_draw() * QS),
            "k": bf(relu_draw() * QS),
            "v": bf(relu_draw() * VS * t[None, :, None, None]),
            "w_up": bf(np.random.standard_normal((C, C)) * 2.0 / np.sqrt(C) / t[None, :]),
            "gamma": bf(np.random.uniform(size=C)),
            "beta": bf(np.random.standard_normal(C) * 0.1),
            "mean": bf(np.random.standard_normal(C) * 0.1),
            "var": bf(np.random.uniform(size=C) + 0.5)}


def reference(q, k, v, w_up, gamma, beta, mean, var):
    qm = f64(q).reshape(B, C, N).transpose(0, 2, 1)
    km = f64(k).reshape(B, C, N)
    vm = f64(v).reshape(B, C, N).transpose(0, 2, 1)
    sim = qm @ km
    e = np.exp(sim - sim.max(-1, keepdims=True))
    ctx = (mxq(e, 2, "e4m3") @ mxq(vm, 1, "e4m3")) / e.sum(-1, keepdims=True)
    ctx_t = ctx.transpose(0, 2, 1)
    y = mxq(f64(w_up), 1, "e4m3") @ mxq(ctx_t, 1, "e4m3")
    a = (f64(gamma) / np.sqrt(f64(var) + EPS))[:, None]
    out = np.maximum((y - f64(mean)[:, None]) * a + f64(beta)[:, None], 0.0)
    return out.reshape(B, C, H, W)

@@ -1,0 +1,314 @@
+from contextlib import ExitStack
+
+import concourse.mybir as mybir
+from concourse.masks import make_identity
+
+F32 = mybir.dt.float32
+BF16 = mybir.dt.bfloat16
+U32 = mybir.dt.uint32
+U8 = mybir.dt.uint8
+FP8X4 = mybir.dt.float8_e4m3fn_x4
+ALU = mybir.AluOpType
+ACT = mybir.ActivationFunctionType
+AXIS = mybir.AxisListType
+
+P = 128
+C = 512
+N = 1024
+PACK = 4
+K_PASS = P * PACK
+BANK = 512
+C_TILES = C // P
+N_TILES = N // P
+M_PASSES = N // K_PASS
+PAIR = 2 * P
+PSUM_BANKS = 8
+EPS = 1e-5
+
+LAG_T = 2
+LAG_X = 6
+LAG_Y = 10
+
+FLOPS = 2 * N * N * C * 2 + 2 * C * C * N
+
+
+def tile_objectattention_pa_kernel(tc, q, k, v, w_up, gamma, beta, mean, var, out):
+    nc = tc.nc
+    with ExitStack() as ctx:
+        ctx.enter_context(tc.manual_schedule())
+        keep = ctx.enter_context(tc.tile_pool(name="keep", bufs=1))
+        ring = ctx.enter_context(tc.tile_pool(name="ring", bufs=3))
+        psum = ctx.enter_context(tc.psum_pool(name="psum", bufs=1))
+
+        banks_handed_out = []
+
+        def psum_bank(shape, dtype):
+            bank = psum.tile(shape, dtype, name="bank", tag="bank%d" % (len(banks_handed_out) % PSUM_BANKS))
+            banks_handed_out.append(bank)
+            return bank
+
+        q_view = q[0].rearrange("(p a) h w -> p a (h w)", a=C_TILES)
+        k_view = k[0].rearrange("(p a) h w -> p a (h w)", a=C_TILES)
+        q_sb = keep.tile([P, C_TILES, N], BF16)
+        k_sb = keep.tile([P, C_TILES, N], BF16)
+        for a in range(C_TILES):
+            nc.sync.dma_start(out=k_sb[:, a, :], in_=k_view[:, a, :])
+            nc.sync.dma_start(out=q_sb[:, a, :], in_=q_view[:, a, :])
+        v_view = v[0].rearrange("(u p b) h w -> p u b (h w)", u=2, b=2)
+        v_sb = keep.tile([P, 2, 2, N], BF16)
+        for u in range(2):
+            nc.sync.dma_start(out=v_sb[:, u, :, :], in_=v_view[:, u, :, :])
+        w_sb = keep.tile([P, C_TILES, C], BF16)
+        nc.sync.dma_start(out=w_sb[:], in_=w_up.rearrange("(p i) c -> p i c", i=C_TILES))
+        out_view = out[0].rearrange("(p i) h w -> p i (h w)", i=C_TILES)
+        gamma_sb = keep.tile([P, C_TILES], BF16)
+        beta_sb = keep.tile([P, C_TILES], BF16)
+        mean_sb = keep.tile([P, C_TILES], BF16)
+        var_sb = keep.tile([P, C_TILES], BF16)
+        nc.scalar.dma_start(out=var_sb[:], in_=var.rearrange("(p i) -> p i", i=C_TILES))
+        nc.scalar.dma_start(out=gamma_sb[:], in_=gamma.rearrange("(p i) -> p i", i=C_TILES))
+        nc.scalar.dma_start(out=mean_sb[:], in_=mean.rearrange("(p i) -> p i", i=C_TILES))
+        nc.scalar.dma_start(out=beta_sb[:], in_=beta.rearrange("(p i) -> p i", i=C_TILES))
+
+        ident_bf = keep.tile([P, P], BF16)
+        make_identity(nc, ident_bf[:])
+        ident_f32 = keep.tile([P, P], F32)
+        make_identity(nc, ident_f32[:])
+
+        var_eps = keep.tile([P, C_TILES], F32)
+        std = keep.tile([P, C_TILES], F32)
+        inv_std = keep.tile([P, C_TILES], F32)
+        bn_scale = keep.tile([P, C_TILES], F32)
+        mean_scaled = keep.tile([P, C_TILES], F32)
+        bn_shift = keep.tile([P, C_TILES], F32)
+        nc.vector.tensor_scalar_add(out=var_eps[:], in0=var_sb[:], scalar1=EPS)
+        nc.scalar.sqrt(out=std[:], in_=var_eps[:])
+        nc.vector.reciprocal(out=inv_std[:], in_=std[:])
+        nc.vector.tensor_mul(out=bn_scale[:], in0=gamma_sb[:], in1=inv_std[:])
+        nc.vector.tensor_mul(out=mean_scaled[:], in0=mean_sb[:], in1=bn_scale[:])
+        nc.vector.tensor_sub(out=bn_shift[:], in0=beta_sb[:], in1=mean_scaled[:])
+
+        v_grouped = keep.tile([P, M_PASSES, C, PACK], BF16, align_bytes=64)
+        v_codes = keep.tile([P, M_PASSES, C], U32, align_bytes=64)
+        v_scales = keep.tile([P, M_PASSES, C], U8, align_bytes=64)
+        w_grouped = keep.tile([P, C, PACK], BF16, align_bytes=64)
+        w_codes = keep.tile([P, C], U32, align_bytes=64)
+        w_scales = keep.tile([P, C], U8, align_bytes=64)
+        e_codes = keep.tile([P, N_TILES, M_PASSES, P], U32, align_bytes=64)
+        e_scales = keep.tile([P, N_TILES, M_PASSES, P], U8, align_bytes=64)
+        inv_sum_bcast = keep.tile([P, N_TILES, P], F32)
+        ctx_codes = keep.tile([P, N], U32, align_bytes=64)
+        ctx_scales = keep.tile([P, N], U8, align_bytes=64)
+        out_sb = keep.tile([P, C_TILES, N], F32)
+
+        score_banks = {}
+        neg_max = {}
+        e_rows = {}
+        e_sums = {}
+        inv_sum = {}
+        eT_banks = {}
+        inv_banks = {}
+        e_grouped = {}
+
+        def open_score_banks(j):
+            score_banks[j] = [psum_bank([P, BANK], F32) for h in range(2)]
+
+        def score_matmul(j, h, a):
+            nc.tensor.matmul(
+                out=score_banks[j][h][:],
+                lhsT=q_sb[:, a, j * P : (j + 1) * P],
+                rhs=k_sb[:, a, h * BANK : (h + 1) * BANK],
+                start=(a == 0),
+                stop=(a == C_TILES - 1),
+            )
+
+        def scores(j):
+            open_score_banks(j)
+            for h in range(2):
+                for a in range(C_TILES):
+                    score_matmul(j, h, a)
+
+        def row_max(j):
+            bank_max = ring.tile([P, 2], F32)
+            for h in range(2):
+                nc.vector.tensor_reduce(
+                    out=bank_max[:, h : h + 1], in_=score_banks[j][h][:], axis=AXIS.X, op=ALU.max
+                )
+            neg = ring.tile([P, 1], F32)
+            nc.vector.tensor_scalar(
+                out=neg[:],
+                in0=bank_max[:, 0:1],
+                scalar1=bank_max[:, 1:2],
+                scalar2=-1.0,
+                op0=ALU.max,
+                op1=ALU.mult,
+            )
+            neg_max[j] = neg
+
+        def exponentials(j):
+            e_row = ring.tile([P, N], BF16)
+            sums = ring.tile([P, 2], F32)
+            for g in range(M_PASSES):
+                nc.scalar.activation(
+                    out=e_row[:, g * BANK : (g + 1) * BANK].rearrange("p (u b i) -> p u b i", u=2, b=2),
+                    in_=score_banks[j][g][:].rearrange("p (u i b) -> p u b i", u=2, b=2),
+                    func=ACT.Exp,
+                    bias=neg_max[j][:, 0:1],
+                    scale=1.0,
+                    accum_out=sums[:, g : g + 1],
+                )
+            e_rows[j] = e_row
+            e_sums[j] = sums
+
+        def reciprocal_of_row_sum(j):
+            total = ring.tile([P, 1], F32)
+            nc.vector.tensor_add(out=total[:], in0=e_sums[j][:, 0:1], in1=e_sums[j][:, 1:2])
+            inv = ring.tile([P, 1], F32)
+            nc.vector.reciprocal(out=inv[:], in_=total[:])
+            inv_sum[j] = inv
+
+        def transpose_e(j):
+            eT = psum_bank([P, M_PASSES * PACK, P], BF16)
+            for x in range(M_PASSES * PACK):
+                nc.tensor.transpose(
+                    out=eT[:, x, :], in_=e_rows[j][:, x * P : (x + 1) * P], identity=ident_bf[:]
+                )
+            eT_banks[j] = eT
+            inv_ps = psum_bank([P, P], F32)
+            nc.tensor.transpose(
+                out=inv_ps[:], in_=inv_sum[j][:, 0:1].to_broadcast([P, P]), identity=ident_f32[:]
+            )
+            inv_banks[j] = inv_ps
+
+        def copy_out_e(j):
+            nc.vector.tensor_copy(out=inv_sum_bcast[:, j, :], in_=inv_banks[j][:])
+            grouped = ring.tile([P, M_PASSES, P, PACK], BF16, align_bytes=64)
+            nc.scalar.copy(out=grouped[:], in_=eT_banks[j][:].rearrange("p (g t) n -> p g n t", t=PACK))
+            e_grouped[j] = grouped
+
+        def quantise_e(j):
+            nc.vector.quantize_mx(
+                out=e_codes[:, j, :, :].rearrange("p g n -> p (g n)").bitcast(FP8X4),
+                scales=e_scales[:, j, :, :].rearrange("p g n -> p (g n)"),
+                in_=e_grouped[j][:].rearrange("p g n t -> p (g n t)"),
+            )
+
+        def context(j):
+            ctx_ps = psum_bank([P, PACK, P], F32)
+            for t in range(PACK):
+                for g in range(M_PASSES):
+                    nc.tensor.matmul_mx(
+                        out=ctx_ps[:, t, :],
+                        lhsT=v_codes[:, g, t * P : (t + 1) * P].bitcast(FP8X4),
+                        lhsT_scale=v_scales[:, g, t * P : (t + 1) * P],
+                        rhs=e_codes[:, j, g, :].bitcast(FP8X4),
+                        rhs_scale=e_scales[:, j, g, :],
+                        start=(g == 0),
+                        stop=(g == M_PASSES - 1),
+                    )
+            ctx_grouped = ring.tile([P, P, PACK], BF16, align_bytes=64)
+            nc.vector.tensor_tensor(
+                out=ctx_grouped[:],
+                in0=ctx_ps[:].rearrange("p t n -> p n t"),
+                in1=inv_sum_bcast[:, j, :].unsqueeze(2).to_broadcast([P, P, PACK]),
+                op=ALU.mult,
+            )
+            nc.vector.quantize_mx(
+                out=ctx_codes[:, j * P : (j + 1) * P].bitcast(FP8X4),
+                scales=ctx_scales[:, j * P : (j + 1) * P],
+                in_=ctx_grouped[:].rearrange("p n t -> p (n t)"),
+            )
+
+        def project(pair, half):
+            cols = slice(pair * PAIR, (pair + 1) * PAIR)
+            y_ps = psum_bank([P, 2, PAIR], F32)
+            for x in range(2):
+                i = 2 * half + x
+                nc.tensor.matmul_mx(
+                    out=y_ps[:, x, :],
+                    lhsT=w_codes[:, i * P : (i + 1) * P].bitcast(FP8X4),
+                    lhsT_scale=w_scales[:, i * P : (i + 1) * P],
+                    rhs=ctx_codes[:, cols].bitcast(FP8X4),
+                    rhs_scale=ctx_scales[:, cols],
+                    start=True,
+                    stop=True,
+                )
+            for x in range(2):
+                i = 2 * half + x
+                nc.scalar.activation(
+                    out=out_sb[:, i, cols],
+                    in_=y_ps[:, x, :],
+                    func=ACT.Relu,
+                    bias=bn_shift[:, i : i + 1],
+                    scale=bn_scale[:, i : i + 1],
+                )
+            tiles = slice(2 * half, 2 * half + 2)
+            nc.sync.dma_start(out=out_view[:, tiles, cols], in_=out_sb[:, tiles, cols])
+
+        def transpose_v(t, copy):
+            words = v_sb[:, t // 2, t % 2, :].bitcast(F32)
+            vT = psum_bank([P, M_PASSES * 2, P], F32)
+            for x in range(M_PASSES * 2):
+                nc.tensor.transpose(out=vT[:, x, :], in_=words[:, x * P : (x + 1) * P], identity=ident_f32[:])
+            copy(
+                out=v_grouped[:].bitcast(F32)[:, :, t * P : (t + 1) * P, :],
+                in_=vT[:].rearrange("p (g u) c -> p g c u", u=2),
+            )
+
+        def transpose_w(half):
+            wT = psum_bank([P, 2, 2, P], F32)
+            for x in range(2):
+                words = w_sb[:, 2 * half + x, :].bitcast(F32)
+                for u in range(2):
+                    nc.tensor.transpose(out=wT[:, x, u, :], in_=words[:, u * P : (u + 1) * P], identity=ident_f32[:])
+            nc.vector.tensor_copy(
+                out=w_grouped[:].bitcast(F32).rearrange("p (i o) u -> p i o u", i=C_TILES)[:, 2 * half : 2 * half + 2, :, :],
+                in_=wT[:].rearrange("p x u o -> p x o u"),
+            )
+
+        def is_tile(j):
+            return 0 <= j < N_TILES
+
+        open_score_banks(0)
+        open_score_banks(1)
+        for a in range(C_TILES):
+            for j in range(2):
+                for h in range(2):
+                    score_matmul(j, h, a)
+
+        for s in range(LAG_Y + 2 * (N // PAIR)):
+            if 2 <= s < N_TILES:
+                scores(s)
+            if is_tile(s):
+                row_max(s)
+            if s >= LAG_Y:
+                project((s - LAG_Y) // 2, (s - LAG_Y) % 2)
+            if is_tile(s - LAG_X):
+                context(s - LAG_X)
+            if is_tile(s - LAG_T):
+                transpose_e(s - LAG_T)
+            if is_tile(s):
+                exponentials(s)
+            if is_tile(s - LAG_T):
+                copy_out_e(s - LAG_T)
+            if is_tile(s - 1):
+                reciprocal_of_row_sum(s - 1)
+            if is_tile(s - LAG_T - 1):
+                quantise_e(s - LAG_T - 1)
+            if s < 2:
+                transpose_v(2 * s, nc.vector.tensor_copy)
+                transpose_v(2 * s + 1, nc.scalar.copy)
+            if s == 2:
+                nc.vector.quantize_mx(
+                    out=v_codes[:].rearrange("p g c -> p (g c)").bitcast(FP8X4),
+                    scales=v_scales[:].rearrange("p g c -> p (g c)"),
+                    in_=v_grouped[:].rearrange("p g c t -> p (g c t)"),
+                )
+            if 2 <= s < 4:
+                transpose_w(s - 2)
+            if s == 4:
+                nc.vector.quantize_mx(
+                    out=w_codes[:].bitcast(FP8X4),
+                    scales=w_scales[:],
+                    in_=w_grouped[:].rearrange("p o t -> p (o t)"),
+                )

@@ -27,7 +27,7 @@ EPS = 1e-5
 
 LAG_T = 2
 LAG_X = 6
-LAG_Y = 10
+LAG_Y = 11
 
 FLOPS = 2 * N * N * C * 2 + 2 * C * C * N
 
@@ -65,28 +65,26 @@ def tile_objectattention_pa_kernel(tc, q, k, v, w_up, gamma, beta, mean, var, ou
         beta_sb = keep.tile([P, C_TILES], BF16)
         mean_sb = keep.tile([P, C_TILES], BF16)
         var_sb = keep.tile([P, C_TILES], BF16)
-        nc.scalar.dma_start(out=var_sb[:], in_=var.rearrange("(p i) -> p i", i=C_TILES))
-        nc.scalar.dma_start(out=gamma_sb[:], in_=gamma.rearrange("(p i) -> p i", i=C_TILES))
-        nc.scalar.dma_start(out=mean_sb[:], in_=mean.rearrange("(p i) -> p i", i=C_TILES))
-        nc.scalar.dma_start(out=beta_sb[:], in_=beta.rearrange("(p i) -> p i", i=C_TILES))
+        nc.sync.dma_start(out=var_sb[:], in_=var.rearrange("(p i) -> p i", i=C_TILES))
+        nc.sync.dma_start(out=gamma_sb[:], in_=gamma.rearrange("(p i) -> p i", i=C_TILES))
+        nc.sync.dma_start(out=mean_sb[:], in_=mean.rearrange("(p i) -> p i", i=C_TILES))
+        nc.sync.dma_start(out=beta_sb[:], in_=beta.rearrange("(p i) -> p i", i=C_TILES))
 
-        ident_bf = keep.tile([P, P], BF16)
-        make_identity(nc, ident_bf[:])
         ident_f32 = keep.tile([P, P], F32)
         make_identity(nc, ident_f32[:])
 
         var_eps = keep.tile([P, C_TILES], F32)
-        std = keep.tile([P, C_TILES], F32)
+        minus_half = keep.tile([P, C_TILES], F32)
         inv_std = keep.tile([P, C_TILES], F32)
         bn_scale = keep.tile([P, C_TILES], F32)
         mean_scaled = keep.tile([P, C_TILES], F32)
         bn_shift = keep.tile([P, C_TILES], F32)
-        nc.vector.tensor_scalar_add(out=var_eps[:], in0=var_sb[:], scalar1=EPS)
-        nc.scalar.sqrt(out=std[:], in_=var_eps[:])
-        nc.vector.reciprocal(out=inv_std[:], in_=std[:])
-        nc.vector.tensor_mul(out=bn_scale[:], in0=gamma_sb[:], in1=inv_std[:])
-        nc.vector.tensor_mul(out=mean_scaled[:], in0=mean_sb[:], in1=bn_scale[:])
-        nc.vector.tensor_sub(out=bn_shift[:], in0=beta_sb[:], in1=mean_scaled[:])
+        nc.gpsimd.memset(minus_half[:], -0.5)
+        nc.gpsimd.tensor_scalar_add(out=var_eps[:], in0=var_sb[:], scalar1=EPS)
+        nc.gpsimd.tensor_tensor(out=inv_std[:], in0=var_eps[:], in1=minus_half[:], op=ALU.pow)
+        nc.gpsimd.tensor_mul(out=bn_scale[:], in0=gamma_sb[:], in1=inv_std[:])
+        nc.gpsimd.tensor_mul(out=mean_scaled[:], in0=mean_sb[:], in1=bn_scale[:])
+        nc.gpsimd.tensor_sub(out=bn_shift[:], in0=beta_sb[:], in1=mean_scaled[:])
 
         v_grouped = keep.tile([P, M_PASSES, C, PACK], BF16, align_bytes=64)
         v_codes = keep.tile([P, M_PASSES, C], U32, align_bytes=64)
@@ -109,6 +107,7 @@ def tile_objectattention_pa_kernel(tc, q, k, v, w_up, gamma, beta, mean, var, ou
         eT_banks = {}
         inv_banks = {}
         e_grouped = {}
+        ctx_grouped = {}
 
         def open_score_banks(j):
             score_banks[j] = [psum_bank([P, BANK], F32) for h in range(2)]
@@ -150,8 +149,8 @@ def tile_objectattention_pa_kernel(tc, q, k, v, w_up, gamma, beta, mean, var, ou
             sums = ring.tile([P, 2], F32)
             for g in range(M_PASSES):
                 nc.scalar.activation(
-                    out=e_row[:, g * BANK : (g + 1) * BANK].rearrange("p (u b i) -> p u b i", u=2, b=2),
-                    in_=score_banks[j][g][:].rearrange("p (u i b) -> p u b i", u=2, b=2),
+                    out=e_row[:, g * BANK : (g + 1) * BANK],
+                    in_=score_banks[j][g][:],
                     func=ACT.Exp,
                     bias=neg_max[j][:, 0:1],
                     scale=1.0,
@@ -168,11 +167,10 @@ def tile_objectattention_pa_kernel(tc, q, k, v, w_up, gamma, beta, mean, var, ou
             inv_sum[j] = inv
 
         def transpose_e(j):
-            eT = psum_bank([P, M_PASSES * PACK, P], BF16)
-            for x in range(M_PASSES * PACK):
-                nc.tensor.transpose(
-                    out=eT[:, x, :], in_=e_rows[j][:, x * P : (x + 1) * P], identity=ident_bf[:]
-                )
+            eT = psum_bank([P, M_PASSES * 2, P], F32)
+            words = e_rows[j][:].bitcast(F32)
+            for x in range(M_PASSES * 2):
+                nc.tensor.transpose(out=eT[:, x, :], in_=words[:, x * P : (x + 1) * P], identity=ident_f32[:])
             eT_banks[j] = eT
             inv_ps = psum_bank([P, P], F32)
             nc.tensor.transpose(
@@ -182,8 +180,8 @@ def tile_objectattention_pa_kernel(tc, q, k, v, w_up, gamma, beta, mean, var, ou
 
         def copy_out_e(j):
             nc.vector.tensor_copy(out=inv_sum_bcast[:, j, :], in_=inv_banks[j][:])
-            grouped = ring.tile([P, M_PASSES, P, PACK], BF16, align_bytes=64)
-            nc.scalar.copy(out=grouped[:], in_=eT_banks[j][:].rearrange("p (g t) n -> p g n t", t=PACK))
+            grouped = ring.tile([P, M_PASSES, P, PACK], BF16, name="e_grouped", align_bytes=64)
+            nc.scalar.copy(out=grouped[:].bitcast(F32), in_=eT_banks[j][:].rearrange("p (g u) n -> p g n u", u=2))
             e_grouped[j] = grouped
 
         def quantise_e(j):
@@ -206,17 +204,20 @@ def tile_objectattention_pa_kernel(tc, q, k, v, w_up, gamma, beta, mean, var, ou
                         start=(g == 0),
                         stop=(g == M_PASSES - 1),
                     )
-            ctx_grouped = ring.tile([P, P, PACK], BF16, align_bytes=64)
+            grouped = ring.tile([P, P, PACK], BF16, name="ctx_grouped", align_bytes=64)
             nc.vector.tensor_tensor(
-                out=ctx_grouped[:],
+                out=grouped[:],
                 in0=ctx_ps[:].rearrange("p t n -> p n t"),
                 in1=inv_sum_bcast[:, j, :].unsqueeze(2).to_broadcast([P, P, PACK]),
                 op=ALU.mult,
             )
+            ctx_grouped[j] = grouped
+
+        def quantise_ctx(j):
             nc.vector.quantize_mx(
                 out=ctx_codes[:, j * P : (j + 1) * P].bitcast(FP8X4),
                 scales=ctx_scales[:, j * P : (j + 1) * P],
-                in_=ctx_grouped[:].rearrange("p n t -> p (n t)"),
+                in_=ctx_grouped[j][:].rearrange("p n t -> p (n t)"),
             )
 
         def project(pair, half):
@@ -285,6 +286,8 @@ def tile_objectattention_pa_kernel(tc, q, k, v, w_up, gamma, beta, mean, var, ou
                 project((s - LAG_Y) // 2, (s - LAG_Y) % 2)
             if is_tile(s - LAG_X):
                 context(s - LAG_X)
+            if is_tile(s - LAG_X - 1):
+                quantise_ctx(s - LAG_X - 1)
             if is_tile(s - LAG_T):
                 transpose_e(s - LAG_T)
             if is_tile(s):

@@ -52,8 +52,9 @@ def tile_objectattention_pa_kernel(tc, q, k, v, w_up, gamma, beta, mean, var, ou
         q_sb = keep.tile([P, C_TILES, N], BF16)
         k_sb = keep.tile([P, C_TILES, N], BF16)
         for a in range(C_TILES):
+            nc.sync.dma_start(out=q_sb[:, a, 0:PAIR], in_=q_view[:, a, 0:PAIR])
             nc.sync.dma_start(out=k_sb[:, a, :], in_=k_view[:, a, :])
-            nc.sync.dma_start(out=q_sb[:, a, :], in_=q_view[:, a, :])
+        nc.sync.dma_start(out=q_sb[:, :, PAIR:N], in_=q_view[:, :, PAIR:N])
         v_view = v[0].rearrange("(u p b) h w -> p u b (h w)", u=2, b=2)
         v_sb = keep.tile([P, 2, 2, N], BF16)
         for u in range(2):
@@ -179,7 +180,7 @@ def tile_objectattention_pa_kernel(tc, q, k, v, w_up, gamma, beta, mean, var, ou
             inv_banks[j] = inv_ps
 
         def copy_out_e(j):
-            nc.vector.tensor_copy(out=inv_sum_bcast[:, j, :], in_=inv_banks[j][:])
+            nc.scalar.copy(out=inv_sum_bcast[:, j, :], in_=inv_banks[j][:])
             grouped = ring.tile([P, M_PASSES, P, PACK], BF16, name="e_grouped", align_bytes=64)
             nc.scalar.copy(out=grouped[:].bitcast(F32), in_=eT_banks[j][:].rearrange("p (g u) n -> p g n u", u=2))
             e_grouped[j] = grouped

@@ -23,6 +23,7 @@ N_TILES = N // P
 M_PASSES = N // K_PASS
 PAIR = 2 * P
 PSUM_BANKS = 8
+WARM_UP = 4
 EPS = 1e-5
 
 LAG_T = 2
@@ -47,6 +48,12 @@ def tile_objectattention_pa_kernel(tc, q, k, v, w_up, gamma, beta, mean, var, ou
             banks_handed_out.append(bank)
             return bank
 
+        zeros = keep.tile([P, BANK], BF16)
+        nc.vector.memset(zeros[:], 0.0)
+        warm_ps = psum_bank([P, BANK], F32)
+        for x in range(WARM_UP):
+            nc.tensor.matmul(out=warm_ps[:], lhsT=zeros[:, 0:P], rhs=zeros[:], start=True, stop=True)
+
         q_view = q[0].rearrange("(p a) h w -> p a (h w)", a=C_TILES)
         k_view = k[0].rearrange("(p a) h w -> p a (h w)", a=C_TILES)
         q_sb = keep.tile([P, C_TILES, N], BF16)
@@ -54,11 +61,11 @@ def tile_objectattention_pa_kernel(tc, q, k, v, w_up, gamma, beta, mean, var, ou
         for a in range(C_TILES):
             nc.sync.dma_start(out=q_sb[:, a, 0:PAIR], in_=q_view[:, a, 0:PAIR])
             nc.sync.dma_start(out=k_sb[:, a, :], in_=k_view[:, a, :])
-        nc.sync.dma_start(out=q_sb[:, :, PAIR:N], in_=q_view[:, :, PAIR:N])
         v_view = v[0].rearrange("(u p b) h w -> p u b (h w)", u=2, b=2)
         v_sb = keep.tile([P, 2, 2, N], BF16)
         for u in range(2):
             nc.sync.dma_start(out=v_sb[:, u, :, :], in_=v_view[:, u, :, :])
+        nc.sync.dma_start(out=q_sb[:, :, PAIR:N], in_=q_view[:, :, PAIR:N])
         w_sb = keep.tile([P, C_TILES, C], BF16)
         nc.sync.dma_start(out=w_sb[:], in_=w_up.rearrange("(p i) c -> p i c", i=C_TILES))
         out_view = out[0].rearrange("(p i) h w -> p i (h w)", i=C_TILES)
@@ -180,10 +187,10 @@ def tile_objectattention_pa_kernel(tc, q, k, v, w_up, gamma, beta, mean, var, ou
             inv_banks[j] = inv_ps
 
         def copy_out_e(j):
-            nc.scalar.copy(out=inv_sum_bcast[:, j, :], in_=inv_banks[j][:])
             grouped = ring.tile([P, M_PASSES, P, PACK], BF16, name="e_grouped", align_bytes=64)
             nc.scalar.copy(out=grouped[:].bitcast(F32), in_=eT_banks[j][:].rearrange("p (g u) n -> p g n u", u=2))
             e_grouped[j] = grouped
+            nc.scalar.copy(out=inv_sum_bcast[:, j, :], in_=inv_banks[j][:])
 
         def quantise_e(j):
             nc.vector.quantize_mx(
@@ -244,8 +251,7 @@ def tile_objectattention_pa_kernel(tc, q, k, v, w_up, gamma, beta, mean, var, ou
                     bias=bn_shift[:, i : i + 1],
                     scale=bn_scale[:, i : i + 1],
                 )
-            tiles = slice(2 * half, 2 * half + 2)
-            nc.sync.dma_start(out=out_view[:, tiles, cols], in_=out_sb[:, tiles, cols])
+                nc.sync.dma_start(out=out_view[:, i, cols], in_=out_sb[:, i, cols])
 
         def transpose_v(t, copy):
             words = v_sb[:, t // 2, t % 2, :].bitcast(F32)

@@ -25,10 +25,12 @@ PAIR = 2 * P
 PSUM_BANKS = 8
 WARM_UP = 4
 EPS = 1e-5
+SB = 6
 
+K = {}
 LAG_T = 2
-LAG_X = 6
-LAG_Y = 11
+LAG_X = 5
+LAG_Y = 8
 
 FLOPS = 2 * N * N * C * 2 + 2 * C * C * N
 
@@ -41,16 +43,18 @@ def tile_objectattention_pa_kernel(tc, q, k, v, w_up, gamma, beta, mean, var, ou
         ring = ctx.enter_context(tc.tile_pool(name="ring", bufs=3))
         psum = ctx.enter_context(tc.psum_pool(name="psum", bufs=1))
 
-        banks_handed_out = []
+        rings = {"s": (0, SB), "t": (SB, 7 - SB), "b": (7, 1)}
+        handed = {"s": 0, "t": 0, "b": 0}
 
-        def psum_bank(shape, dtype):
-            bank = psum.tile(shape, dtype, name="bank", tag="bank%d" % (len(banks_handed_out) % PSUM_BANKS))
-            banks_handed_out.append(bank)
+        def psum_bank(shape, dtype, ring="s"):
+            first, n = rings[ring]
+            bank = psum.tile(shape, dtype, name="bank", tag="bank%d" % (first + handed[ring] % n))
+            handed[ring] += 1
             return bank
 
         zeros = keep.tile([P, BANK], BF16)
         nc.vector.memset(zeros[:], 0.0)
-        warm_ps = psum_bank([P, BANK], F32)
+        warm_ps = psum_bank([P, BANK], F32, "b")
         for x in range(WARM_UP):
             nc.tensor.matmul(out=warm_ps[:], lhsT=zeros[:, 0:P], rhs=zeros[:], start=True, stop=True)
 
@@ -58,25 +62,37 @@ def tile_objectattention_pa_kernel(tc, q, k, v, w_up, gamma, beta, mean, var, ou
         k_view = k[0].rearrange("(p a) h w -> p a (h w)", a=C_TILES)
         q_sb = keep.tile([P, C_TILES, N], BF16)
         k_sb = keep.tile([P, C_TILES, N], BF16)
-        for a in range(C_TILES):
-            nc.sync.dma_start(out=q_sb[:, a, 0:PAIR], in_=q_view[:, a, 0:PAIR])
-            nc.sync.dma_start(out=k_sb[:, a, :], in_=k_view[:, a, :])
-        v_view = v[0].rearrange("(u p b) h w -> p u b (h w)", u=2, b=2)
-        v_sb = keep.tile([P, 2, 2, N], BF16)
-        for u in range(2):
-            nc.sync.dma_start(out=v_sb[:, u, :, :], in_=v_view[:, u, :, :])
+        first, others = slice(0, 1), slice(1, C_TILES)
+        left, right = slice(0, BANK), slice(BANK, N)
+        nc.sync.dma_start(out=q_sb[:, first, 0:PAIR], in_=q_view[:, first, 0:PAIR])
+        nc.sync.dma_start(out=k_sb[:, first, left], in_=k_view[:, first, left])
+        nc.sync.dma_start(out=q_sb[:, others, 0:PAIR], in_=q_view[:, others, 0:PAIR])
+        for a in range(1, C_TILES):
+            nc.sync.dma_start(out=k_sb[:, a, left], in_=k_view[:, a, left])
+        for pair in (slice(0, 2), slice(2, 4)):
+            nc.sync.dma_start(out=k_sb[:, pair, right], in_=k_view[:, pair, right])
         nc.sync.dma_start(out=q_sb[:, :, PAIR:N], in_=q_view[:, :, PAIR:N])
-        w_sb = keep.tile([P, C_TILES, C], BF16)
-        nc.sync.dma_start(out=w_sb[:], in_=w_up.rearrange("(p i) c -> p i c", i=C_TILES))
-        out_view = out[0].rearrange("(p i) h w -> p i (h w)", i=C_TILES)
+        w_raw = keep.tile([P, C // 16, 64], BF16, align_bytes=64)
+        w_view = w_up.rearrange("(y j) (u a k) -> u a j y k", j=16, u=2, a=4)
+        for a in range(4):
+            for u in range(2):
+                nc.sync.dma_start(out=w_raw[32 * a + u : 32 * a + 32 : 2, :, :], in_=w_view[u, a])
+        v_raw = keep.tile([P, M_PASSES, 2, C // 32, 64], BF16, align_bytes=64)
+        v_view = v[0].rearrange("(x j b) (g u a y) w -> b u a j g x (y w)", j=16, b=2, g=2, u=2, a=4)
+        for b in range(2):
+            for a in range(4):
+                for u in range(2):
+                    for g in range(2):
+                        nc.sync.dma_start(out=v_raw[32 * a + u : 32 * a + 32 : 2, g, b, :, :], in_=v_view[b, u, a, :, g])
+        out_view = out[0].rearrange("(i p) h w -> p i (h w)", i=C_TILES)
         gamma_sb = keep.tile([P, C_TILES], BF16)
         beta_sb = keep.tile([P, C_TILES], BF16)
         mean_sb = keep.tile([P, C_TILES], BF16)
         var_sb = keep.tile([P, C_TILES], BF16)
-        nc.sync.dma_start(out=var_sb[:], in_=var.rearrange("(p i) -> p i", i=C_TILES))
-        nc.sync.dma_start(out=gamma_sb[:], in_=gamma.rearrange("(p i) -> p i", i=C_TILES))
-        nc.sync.dma_start(out=mean_sb[:], in_=mean.rearrange("(p i) -> p i", i=C_TILES))
-        nc.sync.dma_start(out=beta_sb[:], in_=beta.rearrange("(p i) -> p i", i=C_TILES))
+        nc.sync.dma_start(out=var_sb[:], in_=var.rearrange("(i p) -> p i", i=C_TILES))
+        nc.sync.dma_start(out=gamma_sb[:], in_=gamma.rearrange("(i p) -> p i", i=C_TILES))
+        nc.sync.dma_start(out=mean_sb[:], in_=mean.rearrange("(i p) -> p i", i=C_TILES))
+        nc.sync.dma_start(out=beta_sb[:], in_=beta.rearrange("(i p) -> p i", i=C_TILES))
 
         ident_f32 = keep.tile([P, P], F32)
         make_identity(nc, ident_f32[:])
@@ -88,12 +104,8 @@ def tile_objectattention_pa_kernel(tc, q, k, v, w_up, gamma, beta, mean, var, ou
         mean_scaled = keep.tile([P, C_TILES], F32)
         bn_shift = keep.tile([P, C_TILES], F32)
         nc.gpsimd.memset(minus_half[:], -0.5)
-        nc.gpsimd.tensor_scalar_add(out=var_eps[:], in0=var_sb[:], scalar1=EPS)
-        nc.gpsimd.tensor_tensor(out=inv_std[:], in0=var_eps[:], in1=minus_half[:], op=ALU.pow)
-        nc.gpsimd.tensor_mul(out=bn_scale[:], in0=gamma_sb[:], in1=inv_std[:])
-        nc.gpsimd.tensor_mul(out=mean_scaled[:], in0=mean_sb[:], in1=bn_scale[:])
-        nc.gpsimd.tensor_sub(out=bn_shift[:], in0=beta_sb[:], in1=mean_scaled[:])
-
+        minus_one = keep.tile([P, 2], F32)
+        nc.gpsimd.memset(minus_one[:], -1.0)
         v_grouped = keep.tile([P, M_PASSES, C, PACK], BF16, align_bytes=64)
         v_codes = keep.tile([P, M_PASSES, C], U32, align_bytes=64)
         v_scales = keep.tile([P, M_PASSES, C], U8, align_bytes=64)
@@ -106,14 +118,17 @@ def tile_objectattention_pa_kernel(tc, q, k, v, w_up, gamma, beta, mean, var, ou
         ctx_codes = keep.tile([P, N], U32, align_bytes=64)
         ctx_scales = keep.tile([P, N], U8, align_bytes=64)
         out_sb = keep.tile([P, C_TILES, N], F32)
+        neg_max = keep.tile([P, N_TILES, M_PASSES], F32)
+        e_sums = keep.tile([P, N_TILES, M_PASSES], F32)
+        row_sums = keep.tile([P, N_TILES], F32)
+        inv_sum = keep.tile([P, N_TILES], F32)
 
         score_banks = {}
-        neg_max = {}
         e_rows = {}
-        e_sums = {}
-        inv_sum = {}
         eT_banks = {}
         inv_banks = {}
+        ctx_banks = {}
+        y_banks = {}
         e_grouped = {}
         ctx_grouped = {}
 
@@ -135,62 +150,61 @@ def tile_objectattention_pa_kernel(tc, q, k, v, w_up, gamma, beta, mean, var, ou
                 for a in range(C_TILES):
                     score_matmul(j, h, a)
 
-        def row_max(j):
-            bank_max = ring.tile([P, 2], F32)
-            for h in range(2):
-                nc.vector.tensor_reduce(
-                    out=bank_max[:, h : h + 1], in_=score_banks[j][h][:], axis=AXIS.X, op=ALU.max
-                )
-            neg = ring.tile([P, 1], F32)
+        def bank_maximum(j, h):
+            negated = ring.tile([P, BANK], BF16)
             nc.vector.tensor_scalar(
-                out=neg[:],
-                in0=bank_max[:, 0:1],
-                scalar1=bank_max[:, 1:2],
-                scalar2=-1.0,
-                op0=ALU.max,
-                op1=ALU.mult,
+                out=negated[:],
+                in0=score_banks[j][h][:],
+                scalar1=-1.0,
+                scalar2=None if h == 0 else neg_max[:, j, 0:1],
+                op0=ALU.mult,
+                op1=ALU.min,
+                accum_out=neg_max[:, j, h : h + 1],
             )
-            neg_max[j] = neg
 
         def exponentials(j):
             e_row = ring.tile([P, N], BF16)
-            sums = ring.tile([P, 2], F32)
             for g in range(M_PASSES):
                 nc.scalar.activation(
                     out=e_row[:, g * BANK : (g + 1) * BANK],
                     in_=score_banks[j][g][:],
                     func=ACT.Exp,
-                    bias=neg_max[j][:, 0:1],
+                    bias=neg_max[:, j, 1:2],
                     scale=1.0,
-                    accum_out=sums[:, g : g + 1],
+                    accum_out=e_sums[:, j, g : g + 1],
                 )
             e_rows[j] = e_row
-            e_sums[j] = sums
 
-        def reciprocal_of_row_sum(j):
-            total = ring.tile([P, 1], F32)
-            nc.vector.tensor_add(out=total[:], in0=e_sums[j][:, 0:1], in1=e_sums[j][:, 1:2])
-            inv = ring.tile([P, 1], F32)
-            nc.vector.reciprocal(out=inv[:], in_=total[:])
-            inv_sum[j] = inv
+        def inverse_sums(j):
+            nc.gpsimd.tensor_tensor(
+                out=row_sums[:, j : j + 2], in0=e_sums[:, j : j + 2, 0], in1=e_sums[:, j : j + 2, 1], op=ALU.add
+            )
+            nc.gpsimd.tensor_tensor(
+                out=inv_sum[:, j : j + 2], in0=row_sums[:, j : j + 2], in1=minus_one[:], op=ALU.pow
+            )
 
         def transpose_e(j):
-            eT = psum_bank([P, M_PASSES * 2, P], F32)
+            eT = psum_bank([P, M_PASSES * 2, P], F32, "t")
             words = e_rows[j][:].bitcast(F32)
             for x in range(M_PASSES * 2):
                 nc.tensor.transpose(out=eT[:, x, :], in_=words[:, x * P : (x + 1) * P], identity=ident_f32[:])
             eT_banks[j] = eT
-            inv_ps = psum_bank([P, P], F32)
-            nc.tensor.transpose(
-                out=inv_ps[:], in_=inv_sum[j][:, 0:1].to_broadcast([P, P]), identity=ident_f32[:]
-            )
+
+        def transpose_inv(j):
+            inv_ps = psum_bank([P, 2, P], F32, "b")
+            for x in range(2):
+                nc.tensor.transpose(
+                    out=inv_ps[:, x, :], in_=inv_sum[:, j + x : j + x + 1].to_broadcast([P, P]), identity=ident_f32[:]
+                )
             inv_banks[j] = inv_ps
 
         def copy_out_e(j):
             grouped = ring.tile([P, M_PASSES, P, PACK], BF16, name="e_grouped", align_bytes=64)
             nc.scalar.copy(out=grouped[:].bitcast(F32), in_=eT_banks[j][:].rearrange("p (g u) n -> p g n u", u=2))
             e_grouped[j] = grouped
-            nc.scalar.copy(out=inv_sum_bcast[:, j, :], in_=inv_banks[j][:])
+
+        def copy_out_inv(j):
+            nc.scalar.copy(out=inv_sum_bcast[:, j : j + 2, :], in_=inv_banks[j][:])
 
         def quantise_e(j):
             nc.vector.quantize_mx(
@@ -212,11 +226,15 @@ def tile_objectattention_pa_kernel(tc, q, k, v, w_up, gamma, beta, mean, var, ou
                         start=(g == 0),
                         stop=(g == M_PASSES - 1),
                     )
+            ctx_banks[j] = ctx_ps
+
+        def divide(j):
+            ctx_ps = ctx_banks[j]
             grouped = ring.tile([P, P, PACK], BF16, name="ctx_grouped", align_bytes=64)
             nc.vector.tensor_tensor(
-                out=grouped[:],
-                in0=ctx_ps[:].rearrange("p t n -> p n t"),
-                in1=inv_sum_bcast[:, j, :].unsqueeze(2).to_broadcast([P, P, PACK]),
+                out=grouped[:].rearrange("p n (u b) -> p n u b", b=2),
+                in0=ctx_ps[:].rearrange("p (b u) n -> p n u b", b=2),
+                in1=inv_sum_bcast[:, j, :].unsqueeze(2).unsqueeze(3).to_broadcast([P, P, 2, 2]),
                 op=ALU.mult,
             )
             ctx_grouped[j] = grouped
@@ -242,6 +260,11 @@ def tile_objectattention_pa_kernel(tc, q, k, v, w_up, gamma, beta, mean, var, ou
                     start=True,
                     stop=True,
                 )
+            y_banks[pair, half] = y_ps
+
+        def finish(pair, half):
+            cols = slice(pair * PAIR, (pair + 1) * PAIR)
+            y_ps = y_banks[pair, half]
             for x in range(2):
                 i = 2 * half + x
                 nc.scalar.activation(
@@ -253,72 +276,110 @@ def tile_objectattention_pa_kernel(tc, q, k, v, w_up, gamma, beta, mean, var, ou
                 )
                 nc.sync.dma_start(out=out_view[:, i, cols], in_=out_sb[:, i, cols])
 
-        def transpose_v(t, copy):
-            words = v_sb[:, t // 2, t % 2, :].bitcast(F32)
-            vT = psum_bank([P, M_PASSES * 2, P], F32)
-            for x in range(M_PASSES * 2):
-                nc.tensor.transpose(out=vT[:, x, :], in_=words[:, x * P : (x + 1) * P], identity=ident_f32[:])
-            copy(
-                out=v_grouped[:].bitcast(F32)[:, :, t * P : (t + 1) * P, :],
-                in_=vT[:].rearrange("p (g u) c -> p g c u", u=2),
+        def transpose_v(g, b):
+            half = slice(b * C // 2, (b + 1) * C // 2)
+            nc.vector.transpose(
+                out=v_grouped[:, g, half, :].rearrange("p c t -> p (c t)").bitcast(F32),
+                in_=v_raw[:, g, b, :, :].rearrange("p x k -> p (x k)").bitcast(F32),
+            )
+
+        def quantise_v(g):
+            nc.vector.quantize_mx(
+                out=v_codes[:, g, :].bitcast(FP8X4),
+                scales=v_scales[:, g, :],
+                in_=v_grouped[:, g, :, :].rearrange("p c t -> p (c t)"),
             )
 
         def transpose_w(half):
-            wT = psum_bank([P, 2, 2, P], F32)
-            for x in range(2):
-                words = w_sb[:, 2 * half + x, :].bitcast(F32)
-                for u in range(2):
-                    nc.tensor.transpose(out=wT[:, x, u, :], in_=words[:, u * P : (u + 1) * P], identity=ident_f32[:])
-            nc.vector.tensor_copy(
-                out=w_grouped[:].bitcast(F32).rearrange("p (i o) u -> p i o u", i=C_TILES)[:, 2 * half : 2 * half + 2, :, :],
-                in_=wT[:].rearrange("p x u o -> p x o u"),
+            rows = slice(half * C // 2, (half + 1) * C // 2)
+            blocks = slice(half * C // 32, (half + 1) * C // 32)
+            nc.vector.transpose(
+                out=w_grouped[:, rows, :].rearrange("p o t -> p (o t)").bitcast(F32),
+                in_=w_raw[:, blocks, :].rearrange("p y k -> p (y k)").bitcast(F32),
             )
+
+        def quantise_w():
+            nc.vector.quantize_mx(
+                out=w_codes[:].bitcast(FP8X4),
+                scales=w_scales[:],
+                in_=w_grouped[:].rearrange("p o t -> p (o t)"),
+            )
+
+        def batch_norm():
+            nc.gpsimd.tensor_scalar_add(out=var_eps[:], in0=var_sb[:], scalar1=EPS)
+            nc.gpsimd.tensor_tensor(out=inv_std[:], in0=var_eps[:], in1=minus_half[:], op=ALU.pow)
+            nc.gpsimd.tensor_mul(out=bn_scale[:], in0=gamma_sb[:], in1=inv_std[:])
+            nc.gpsimd.tensor_mul(out=mean_scaled[:], in0=mean_sb[:], in1=bn_scale[:])
+            nc.gpsimd.tensor_sub(out=bn_shift[:], in0=beta_sb[:], in1=mean_scaled[:])
 
         def is_tile(j):
             return 0 <= j < N_TILES
 
+        T, C_, Q, E, X, Y, Z = transpose_e, copy_out_e, quantise_e, exponentials, context, divide, quantise_ctx
+        PR, L, I, B, D = project, finish, inverse_sums, transpose_inv, copy_out_inv
+        BETWEEN = {
+            3: [(transpose_w, (0,))],
+            4: [(transpose_w, (1,))],
+            5: [(transpose_v, (0, 0))],
+            6: [(transpose_v, (0, 1))],
+            7: [(quantise_v, (0,))],
+        }
+        AFTER = {
+            3: [(quantise_e, (0,))],
+            4: [(quantise_e, (1,)), (quantise_w, ())],
+            5: [(quantise_e, (2,)), (transpose_v, (1, 0))],
+            6: [(quantise_e, (3,)), (transpose_v, (1, 1))],
+            7: [(quantise_v, (1,)), (quantise_e, (4,))],
+        }
+        TAIL = [
+[(X, (0,)), (X, (1,)), (Y, (0,)), (Q, (5,)), (Y, (1,)), (Z, (0,)), (I, (6,))],
+            [(T, (6,)), (B, (4,)), (C_, (6,)), (D, (4,)), (X, (2,)), (X, (3,)), (Y, (2,)), (Z, (1,)), (Q, (6,)), (Y, (3,)), (Z, (2,))],
+            [(T, (7,)), (B, (6,)), (C_, (7,)), (D, (6,)), (PR, (0, 0)), (PR, (0, 1)), (L, (0, 0)), (L, (0, 1)), (X, (4,)), (Z, (3,)), (Y, (4,)),  (Q, (7,)), (X, (5,)), (Y, (5,)), (Z, (4,))],
+            [(PR, (1, 0)), (PR, (1, 1)), (L, (1, 0)), (L, (1, 1)), (X, (6,)), (X, (7,)), (Y, (6,)), (Z, (5,)), (Y, (7,)), (Z, (6,)), (PR, (2, 0)), (PR, (2, 1)), (L, (2, 0)), (L, (2, 1)), (Z, (7,))],
+            [(PR, (3, 0)), (PR, (3, 1)), (L, (3, 0)), (L, (3, 1))],
+        ]
         open_score_banks(0)
         open_score_banks(1)
         for a in range(C_TILES):
             for j in range(2):
-                for h in range(2):
-                    score_matmul(j, h, a)
+                score_matmul(j, 0, a)
+        for j in range(2):
+            for a in range(C_TILES):
+                score_matmul(j, 1, a)
 
-        for s in range(LAG_Y + 2 * (N // PAIR)):
-            if 2 <= s < N_TILES:
-                scores(s)
-            if is_tile(s):
-                row_max(s)
-            if s >= LAG_Y:
-                project((s - LAG_Y) // 2, (s - LAG_Y) % 2)
-            if is_tile(s - LAG_X):
-                context(s - LAG_X)
-            if is_tile(s - LAG_X - 1):
-                quantise_ctx(s - LAG_X - 1)
-            if is_tile(s - LAG_T):
-                transpose_e(s - LAG_T)
-            if is_tile(s):
-                exponentials(s)
-            if is_tile(s - LAG_T):
-                copy_out_e(s - LAG_T)
-            if is_tile(s - 1):
-                reciprocal_of_row_sum(s - 1)
-            if is_tile(s - LAG_T - 1):
-                quantise_e(s - LAG_T - 1)
-            if s < 2:
-                transpose_v(2 * s, nc.vector.tensor_copy)
-                transpose_v(2 * s + 1, nc.scalar.copy)
-            if s == 2:
-                nc.vector.quantize_mx(
-                    out=v_codes[:].rearrange("p g c -> p (g c)").bitcast(FP8X4),
-                    scales=v_scales[:].rearrange("p g c -> p (g c)"),
-                    in_=v_grouped[:].rearrange("p g c t -> p (g c t)"),
-                )
-            if 2 <= s < 4:
-                transpose_w(s - 2)
-            if s == 4:
-                nc.vector.quantize_mx(
-                    out=w_codes[:].bitcast(FP8X4),
-                    scales=w_scales[:],
-                    in_=w_grouped[:].rearrange("p o t -> p (o t)"),
-                )
+
+        def run(plan):
+            for call, args in plan:
+                call(*args)
+
+        bank_maximum(0, 0)
+        bank_maximum(1, 0)
+        bank_maximum(0, 1)
+        exponentials(0)
+        bank_maximum(1, 1)
+        exponentials(1)
+        for s in range(2, N_TILES):
+            open_score_banks(s)
+            for a in range(C_TILES):
+                score_matmul(s, 0, a)
+            bank_maximum(s, 0)
+            for call, args in BETWEEN.get(s, ()):
+                call(*args)
+            for a in range(C_TILES):
+                score_matmul(s, 1, a)
+            bank_maximum(s, 1)
+            if s in (4, 6):
+                transpose_inv(s - 4)
+            transpose_e(s - 2)
+            copy_out_e(s - 2)
+            if s in (4, 6):
+                copy_out_inv(s - 4)
+            exponentials(s)
+            if s in (3, 5, 7):
+                inverse_sums(s - 3)
+            for call, args in AFTER.get(s, ()):
+                call(*args)
+        batch_norm()
+        for step in TAIL:
+            for call, args in step:
+                call(*args)

@@ -27,7 +27,6 @@ WARM_UP = 4
 EPS = 1e-5
 SB = 6
 
-K = {}
 LAG_T = 2
 LAG_X = 5
 LAG_Y = 8
@@ -43,18 +42,16 @@ def tile_objectattention_pa_kernel(tc, q, k, v, w_up, gamma, beta, mean, var, ou
         ring = ctx.enter_context(tc.tile_pool(name="ring", bufs=3))
         psum = ctx.enter_context(tc.psum_pool(name="psum", bufs=1))
 
-        rings = {"s": (0, SB), "t": (SB, 7 - SB), "b": (7, 1)}
-        handed = {"s": 0, "t": 0, "b": 0}
+        banks_handed_out = []
 
         def psum_bank(shape, dtype, ring="s"):
-            first, n = rings[ring]
-            bank = psum.tile(shape, dtype, name="bank", tag="bank%d" % (first + handed[ring] % n))
-            handed[ring] += 1
+            bank = psum.tile(shape, dtype, name="bank", tag="bank%d" % (len(banks_handed_out) % PSUM_BANKS))
+            banks_handed_out.append(bank)
             return bank
 
         zeros = keep.tile([P, BANK], BF16)
         nc.vector.memset(zeros[:], 0.0)
-        warm_ps = psum_bank([P, BANK], F32, "b")
+        warm_ps = psum_bank([P, BANK], F32, "t")
         for x in range(WARM_UP):
             nc.tensor.matmul(out=warm_ps[:], lhsT=zeros[:, 0:P], rhs=zeros[:], start=True, stop=True)
 
@@ -62,28 +59,23 @@ def tile_objectattention_pa_kernel(tc, q, k, v, w_up, gamma, beta, mean, var, ou
         k_view = k[0].rearrange("(p a) h w -> p a (h w)", a=C_TILES)
         q_sb = keep.tile([P, C_TILES, N], BF16)
         k_sb = keep.tile([P, C_TILES, N], BF16)
-        first, others = slice(0, 1), slice(1, C_TILES)
         left, right = slice(0, BANK), slice(BANK, N)
-        nc.sync.dma_start(out=q_sb[:, first, 0:PAIR], in_=q_view[:, first, 0:PAIR])
-        nc.sync.dma_start(out=k_sb[:, first, left], in_=k_view[:, first, left])
-        nc.sync.dma_start(out=q_sb[:, others, 0:PAIR], in_=q_view[:, others, 0:PAIR])
+        nc.sync.dma_start(out=q_sb[:, 0, 0:PAIR], in_=q_view[:, 0, 0:PAIR])
+        nc.sync.dma_start(out=k_sb[:, 0, left], in_=k_view[:, 0, left])
+        nc.sync.dma_start(out=k_sb[:, 0, right], in_=k_view[:, 0, right])
         for a in range(1, C_TILES):
-            nc.sync.dma_start(out=k_sb[:, a, left], in_=k_view[:, a, left])
-        for pair in (slice(0, 2), slice(2, 4)):
-            nc.sync.dma_start(out=k_sb[:, pair, right], in_=k_view[:, pair, right])
+            nc.sync.dma_start(out=q_sb[:, a, 0:PAIR], in_=q_view[:, a, 0:PAIR])
+            nc.sync.dma_start(out=k_sb[:, a, :], in_=k_view[:, a, :])
         nc.sync.dma_start(out=q_sb[:, :, PAIR:N], in_=q_view[:, :, PAIR:N])
+        v_view = v[0].rearrange("(u p b) h w -> p u b (h w)", u=2, b=2)
+        v_sb = keep.tile([P, 2, 2, N], BF16)
+        for u in range(2):
+            nc.sync.dma_start(out=v_sb[:, u, :, :], in_=v_view[:, u, :, :])
         w_raw = keep.tile([P, C // 16, 64], BF16, align_bytes=64)
         w_view = w_up.rearrange("(y j) (u a k) -> u a j y k", j=16, u=2, a=4)
-        for a in range(4):
-            for u in range(2):
-                nc.sync.dma_start(out=w_raw[32 * a + u : 32 * a + 32 : 2, :, :], in_=w_view[u, a])
-        v_raw = keep.tile([P, M_PASSES, 2, C // 32, 64], BF16, align_bytes=64)
-        v_view = v[0].rearrange("(x j b) (g u a y) w -> b u a j g x (y w)", j=16, b=2, g=2, u=2, a=4)
-        for b in range(2):
+        for u in range(2):
             for a in range(4):
-                for u in range(2):
-                    for g in range(2):
-                        nc.sync.dma_start(out=v_raw[32 * a + u : 32 * a + 32 : 2, g, b, :, :], in_=v_view[b, u, a, :, g])
+                nc.sync.dma_start(out=w_raw[32 * a + u : 32 * a + 32 : 2, :, :], in_=w_view[u, a])
         out_view = out[0].rearrange("(i p) h w -> p i (h w)", i=C_TILES)
         gamma_sb = keep.tile([P, C_TILES], BF16)
         beta_sb = keep.tile([P, C_TILES], BF16)
@@ -191,7 +183,7 @@ def tile_objectattention_pa_kernel(tc, q, k, v, w_up, gamma, beta, mean, var, ou
             eT_banks[j] = eT
 
         def transpose_inv(j):
-            inv_ps = psum_bank([P, 2, P], F32, "b")
+            inv_ps = psum_bank([P, 2, P], F32, "s")
             for x in range(2):
                 nc.tensor.transpose(
                     out=inv_ps[:, x, :], in_=inv_sum[:, j + x : j + x + 1].to_broadcast([P, P]), identity=ident_f32[:]
@@ -232,9 +224,9 @@ def tile_objectattention_pa_kernel(tc, q, k, v, w_up, gamma, beta, mean, var, ou
             ctx_ps = ctx_banks[j]
             grouped = ring.tile([P, P, PACK], BF16, name="ctx_grouped", align_bytes=64)
             nc.vector.tensor_tensor(
-                out=grouped[:].rearrange("p n (u b) -> p n u b", b=2),
-                in0=ctx_ps[:].rearrange("p (b u) n -> p n u b", b=2),
-                in1=inv_sum_bcast[:, j, :].unsqueeze(2).unsqueeze(3).to_broadcast([P, P, 2, 2]),
+                out=grouped[:],
+                in0=ctx_ps[:].rearrange("p t n -> p n t"),
+                in1=inv_sum_bcast[:, j, :].unsqueeze(2).to_broadcast([P, P, PACK]),
                 op=ALU.mult,
             )
             ctx_grouped[j] = grouped
@@ -276,11 +268,53 @@ def tile_objectattention_pa_kernel(tc, q, k, v, w_up, gamma, beta, mean, var, ou
                 )
                 nc.sync.dma_start(out=out_view[:, i, cols], in_=out_sb[:, i, cols])
 
-        def transpose_v(g, b):
-            half = slice(b * C // 2, (b + 1) * C // 2)
-            nc.vector.transpose(
-                out=v_grouped[:, g, half, :].rearrange("p c t -> p (c t)").bitcast(F32),
-                in_=v_raw[:, g, b, :, :].rearrange("p x k -> p (x k)").bitcast(F32),
+        def project_tile(j):
+            cols = slice(j * P, (j + 1) * P)
+            y_ps = psum_bank([P, C_TILES, P], F32)
+            for i in range(C_TILES):
+                nc.tensor.matmul_mx(
+                    out=y_ps[:, i, :],
+                    lhsT=w_codes[:, i * P : (i + 1) * P].bitcast(FP8X4),
+                    lhsT_scale=w_scales[:, i * P : (i + 1) * P],
+                    rhs=ctx_codes[:, cols].bitcast(FP8X4),
+                    rhs_scale=ctx_scales[:, cols],
+                    start=True,
+                    stop=True,
+                )
+            y_banks[j] = y_ps
+
+        def finish_tile(j):
+            cols = slice(j * P, (j + 1) * P)
+            y_ps = y_banks[j]
+            for i in (0, 1):
+                nc.scalar.activation(
+                    out=out_sb[:, i, cols],
+                    in_=y_ps[:, i, :],
+                    func=ACT.Relu,
+                    bias=bn_shift[:, i : i + 1],
+                    scale=bn_scale[:, i : i + 1],
+                )
+            for i in (2, 3):
+                nc.vector.tensor_scalar(
+                    out=out_sb[:, i, cols],
+                    in0=y_ps[:, i, :],
+                    scalar1=bn_scale[:, i : i + 1],
+                    scalar2=bn_shift[:, i : i + 1],
+                    op0=ALU.mult,
+                    op1=ALU.add,
+                )
+            nc.vector.tensor_scalar_max(out=out_sb[:, 2:4, cols], in0=out_sb[:, 2:4, cols], scalar1=0.0)
+            for half in (slice(0, 2), slice(2, 4)):
+                nc.sync.dma_start(out=out_view[:, half, cols], in_=out_sb[:, half, cols])
+
+        def transpose_v(t, copy):
+            words = v_sb[:, t // 2, t % 2, :].bitcast(F32)
+            vT = psum_bank([P, M_PASSES * 2, P], F32, "t")
+            for x in range(M_PASSES * 2):
+                nc.tensor.transpose(out=vT[:, x, :], in_=words[:, x * P : (x + 1) * P], identity=ident_f32[:])
+            copy(
+                out=v_grouped[:].bitcast(F32)[:, :, t * P : (t + 1) * P, :],
+                in_=vT[:].rearrange("p (g u) c -> p g c u", u=2),
             )
 
         def quantise_v(g):
@@ -316,70 +350,53 @@ def tile_objectattention_pa_kernel(tc, q, k, v, w_up, gamma, beta, mean, var, ou
             return 0 <= j < N_TILES
 
         T, C_, Q, E, X, Y, Z = transpose_e, copy_out_e, quantise_e, exponentials, context, divide, quantise_ctx
+        PT, LT = project_tile, finish_tile
         PR, L, I, B, D = project, finish, inverse_sums, transpose_inv, copy_out_inv
-        BETWEEN = {
-            3: [(transpose_w, (0,))],
-            4: [(transpose_w, (1,))],
-            5: [(transpose_v, (0, 0))],
-            6: [(transpose_v, (0, 1))],
-            7: [(quantise_v, (0,))],
-        }
-        AFTER = {
-            3: [(quantise_e, (0,))],
-            4: [(quantise_e, (1,)), (quantise_w, ())],
-            5: [(quantise_e, (2,)), (transpose_v, (1, 0))],
-            6: [(quantise_e, (3,)), (transpose_v, (1, 1))],
-            7: [(quantise_v, (1,)), (quantise_e, (4,))],
-        }
-        TAIL = [
-[(X, (0,)), (X, (1,)), (Y, (0,)), (Q, (5,)), (Y, (1,)), (Z, (0,)), (I, (6,))],
-            [(T, (6,)), (B, (4,)), (C_, (6,)), (D, (4,)), (X, (2,)), (X, (3,)), (Y, (2,)), (Z, (1,)), (Q, (6,)), (Y, (3,)), (Z, (2,))],
-            [(T, (7,)), (B, (6,)), (C_, (7,)), (D, (6,)), (PR, (0, 0)), (PR, (0, 1)), (L, (0, 0)), (L, (0, 1)), (X, (4,)), (Z, (3,)), (Y, (4,)),  (Q, (7,)), (X, (5,)), (Y, (5,)), (Z, (4,))],
-            [(PR, (1, 0)), (PR, (1, 1)), (L, (1, 0)), (L, (1, 1)), (X, (6,)), (X, (7,)), (Y, (6,)), (Z, (5,)), (Y, (7,)), (Z, (6,)), (PR, (2, 0)), (PR, (2, 1)), (L, (2, 0)), (L, (2, 1)), (Z, (7,))],
-            [(PR, (3, 0)), (PR, (3, 1)), (L, (3, 0)), (L, (3, 1))],
-        ]
         open_score_banks(0)
         open_score_banks(1)
         for a in range(C_TILES):
-            for j in range(2):
-                score_matmul(j, 0, a)
+            for h in range(2):
+                for j in range(2):
+                    score_matmul(j, h, a)
+
+        vcopy = nc.vector.tensor_copy
         for j in range(2):
-            for a in range(C_TILES):
-                score_matmul(j, 1, a)
-
-
-        def run(plan):
-            for call, args in plan:
-                call(*args)
-
-        bank_maximum(0, 0)
-        bank_maximum(1, 0)
-        bank_maximum(0, 1)
-        exponentials(0)
-        bank_maximum(1, 1)
-        exponentials(1)
+            bank_maximum(j, 0)
+            bank_maximum(j, 1)
+            exponentials(j)
         for s in range(2, N_TILES):
-            open_score_banks(s)
-            for a in range(C_TILES):
-                score_matmul(s, 0, a)
+            scores(s)
             bank_maximum(s, 0)
-            for call, args in BETWEEN.get(s, ()):
-                call(*args)
-            for a in range(C_TILES):
-                score_matmul(s, 1, a)
+            if s in (4, 5):
+                quantise_v(s - 4)
+            else:
+                if s >= 6:
+                    transpose_w(s - 6)
             bank_maximum(s, 1)
-            if s in (4, 6):
-                transpose_inv(s - 4)
             transpose_e(s - 2)
             copy_out_e(s - 2)
-            if s in (4, 6):
-                copy_out_inv(s - 4)
+            if s < 4:
+                transpose_v(2 * s - 4, nc.vector.tensor_copy)
+            if s in (5, 7):
+                transpose_inv(s - 5)
+                copy_out_inv(s - 5)
             exponentials(s)
+            if s < 4:
+                transpose_v(2 * s - 3, nc.scalar.copy)
+            quantise_e(s - 2)
+            if s >= 6:
+                context(s - 6)
+                divide(s - 6)
             if s in (3, 5, 7):
                 inverse_sums(s - 3)
-            for call, args in AFTER.get(s, ()):
-                call(*args)
+        quantise_ctx(0)
         batch_norm()
+        TAIL = [
+            [(T, (6,)), (C_, (6,)), (I, (6,)), (X, (2,)), (quantise_w, ()), (Z, (1,)), (Q, (6,)), (Y, (2,)), (X, (3,)), (Z, (2,)), (Y, (3,))],
+            [(B, (4,)), (T, (7,)), (D, (4,)), (C_, (7,)), (PR, (0, 0)), (PR, (0, 1)), (Z, (3,)), (L, (0, 0)), (X, (4,)), (Q, (7,)), (Y, (4,)), (L, (0, 1)), (X, (5,)), (B, (6,)), (D, (6,)), (Z, (4,)), (Y, (5,))],
+            [(PR, (1, 0)), (PR, (1, 1)), (L, (1, 0)), (L, (1, 1)), (X, (6,)), (Z, (5,)), (Y, (6,)), (X, (7,)), (Z, (6,)), (Y, (7,)), (PR, (2, 0)), (PR, (2, 1)), (L, (2, 0)), (L, (2, 1)), (PT, (6,)), (Z, (7,)), (LT, (6,))],
+            [(PT, (7,)), (LT, (7,))],
+        ]
         for step in TAIL:
             for call, args in step:
                 call(*args)

@@ -71,12 +71,6 @@ def tile_objectattention_pa_kernel(tc, q, k, v, w_up, gamma, beta, mean, var, ou
         v_sb = keep.tile([P, 2, 2, N], BF16)
         for u in range(2):
             nc.sync.dma_start(out=v_sb[:, u, :, :], in_=v_view[:, u, :, :])
-        w_raw = keep.tile([P, C // 16, 64], BF16, align_bytes=64)
-        w_view = w_up.rearrange("(y j) (u a k) -> u a j y k", j=16, u=2, a=4)
-        for u in range(2):
-            for a in range(4):
-                nc.sync.dma_start(out=w_raw[32 * a + u : 32 * a + 32 : 2, :, :], in_=w_view[u, a])
-        out_view = out[0].rearrange("(i p) h w -> p i (h w)", i=C_TILES)
         gamma_sb = keep.tile([P, C_TILES], BF16)
         beta_sb = keep.tile([P, C_TILES], BF16)
         mean_sb = keep.tile([P, C_TILES], BF16)
@@ -85,7 +79,12 @@ def tile_objectattention_pa_kernel(tc, q, k, v, w_up, gamma, beta, mean, var, ou
         nc.sync.dma_start(out=gamma_sb[:], in_=gamma.rearrange("(i p) -> p i", i=C_TILES))
         nc.sync.dma_start(out=mean_sb[:], in_=mean.rearrange("(i p) -> p i", i=C_TILES))
         nc.sync.dma_start(out=beta_sb[:], in_=beta.rearrange("(i p) -> p i", i=C_TILES))
-
+        w_raw = keep.tile([P, C // 16, 64], BF16, align_bytes=64)
+        w_view = w_up.rearrange("(y j) (u a k) -> u a j y k", j=16, u=2, a=4)
+        for u in range(2):
+            for a in range(4):
+                nc.sync.dma_start(out=w_raw[32 * a + u : 32 * a + 32 : 2, :, :], in_=w_view[u, a])
+        out_view = out[0].rearrange("(i p) h w -> p i (h w)", i=C_TILES)
         ident_f32 = keep.tile([P, P], F32)
         make_identity(nc, ident_f32[:])
 
@@ -96,8 +95,6 @@ def tile_objectattention_pa_kernel(tc, q, k, v, w_up, gamma, beta, mean, var, ou
         mean_scaled = keep.tile([P, C_TILES], F32)
         bn_shift = keep.tile([P, C_TILES], F32)
         nc.gpsimd.memset(minus_half[:], -0.5)
-        minus_one = keep.tile([P, 2], F32)
-        nc.gpsimd.memset(minus_one[:], -1.0)
         v_grouped = keep.tile([P, M_PASSES, C, PACK], BF16, align_bytes=64)
         v_codes = keep.tile([P, M_PASSES, C], U32, align_bytes=64)
         v_scales = keep.tile([P, M_PASSES, C], U8, align_bytes=64)
@@ -167,13 +164,11 @@ def tile_objectattention_pa_kernel(tc, q, k, v, w_up, gamma, beta, mean, var, ou
                 )
             e_rows[j] = e_row
 
+        def row_sums_of(j):
+            nc.vector.tensor_add(out=row_sums[:, j : j + 2], in0=e_sums[:, j : j + 2, 0], in1=e_sums[:, j : j + 2, 1])
+
         def inverse_sums(j):
-            nc.gpsimd.tensor_tensor(
-                out=row_sums[:, j : j + 2], in0=e_sums[:, j : j + 2, 0], in1=e_sums[:, j : j + 2, 1], op=ALU.add
-            )
-            nc.gpsimd.tensor_tensor(
-                out=inv_sum[:, j : j + 2], in0=row_sums[:, j : j + 2], in1=minus_one[:], op=ALU.pow
-            )
+            nc.vector.reciprocal(out=inv_sum[:, j : j + 2], in_=row_sums[:, j : j + 2])
 
         def transpose_e(j):
             eT = psum_bank([P, M_PASSES * 2, P], F32, "t")
@@ -351,7 +346,9 @@ def tile_objectattention_pa_kernel(tc, q, k, v, w_up, gamma, beta, mean, var, ou
 
         T, C_, Q, E, X, Y, Z = transpose_e, copy_out_e, quantise_e, exponentials, context, divide, quantise_ctx
         PT, LT = project_tile, finish_tile
+        R = row_sums_of
         PR, L, I, B, D = project, finish, inverse_sums, transpose_inv, copy_out_inv
+        batch_norm()
         open_score_banks(0)
         open_score_banks(1)
         for a in range(C_TILES):
@@ -372,7 +369,11 @@ def tile_objectattention_pa_kernel(tc, q, k, v, w_up, gamma, beta, mean, var, ou
             else:
                 if s >= 6:
                     transpose_w(s - 6)
+            if s in (4, 6):
+                row_sums_of(s - 4)
             bank_maximum(s, 1)
+            if s in (4, 6):
+                inverse_sums(s - 4)
             transpose_e(s - 2)
             copy_out_e(s - 2)
             if s < 4:
@@ -387,13 +388,10 @@ def tile_objectattention_pa_kernel(tc, q, k, v, w_up, gamma, beta, mean, var, ou
             if s >= 6:
                 context(s - 6)
                 divide(s - 6)
-            if s in (3, 5, 7):
-                inverse_sums(s - 3)
         quantise_ctx(0)
-        batch_norm()
         TAIL = [
-            [(T, (6,)), (C_, (6,)), (I, (6,)), (X, (2,)), (quantise_w, ()), (Z, (1,)), (Q, (6,)), (Y, (2,)), (X, (3,)), (Z, (2,)), (Y, (3,))],
-            [(B, (4,)), (T, (7,)), (D, (4,)), (C_, (7,)), (PR, (0, 0)), (PR, (0, 1)), (Z, (3,)), (L, (0, 0)), (X, (4,)), (Q, (7,)), (Y, (4,)), (L, (0, 1)), (X, (5,)), (B, (6,)), (D, (6,)), (Z, (4,)), (Y, (5,))],
+            [(R, (4,)), (T, (6,)), (C_, (6,)), (X, (2,)), (quantise_w, ()), (I, (4,)), (Z, (1,)), (Q, (6,)), (Y, (2,)), (X, (3,)), (Z, (2,)), (Y, (3,))],
+            [(B, (4,)), (T, (7,)), (D, (4,)), (C_, (7,)), (PR, (0, 0)), (PR, (0, 1)), (R, (6,)), (Z, (3,)), (I, (6,)), (L, (0, 0)), (X, (4,)), (Q, (7,)), (Y, (4,)), (L, (0, 1)), (X, (5,)), (B, (6,)), (D, (6,)), (Z, (4,)), (Y, (5,))],
             [(PR, (1, 0)), (PR, (1, 1)), (L, (1, 0)), (L, (1, 1)), (X, (6,)), (Z, (5,)), (Y, (6,)), (X, (7,)), (Z, (6,)), (Y, (7,)), (PR, (2, 0)), (PR, (2, 1)), (L, (2, 0)), (L, (2, 1)), (PT, (6,)), (Z, (7,)), (LT, (6,))],
             [(PT, (7,)), (LT, (7,))],
         ]

@@ -42,11 +42,13 @@ def tile_objectattention_pa_kernel(tc, q, k, v, w_up, gamma, beta, mean, var, ou
         ring = ctx.enter_context(tc.tile_pool(name="ring", bufs=3))
         psum = ctx.enter_context(tc.psum_pool(name="psum", bufs=1))
 
-        banks_handed_out = []
+        rings = {"s": (0, SB), "t": (SB, PSUM_BANKS - SB)}
+        handed = {"s": 0, "t": 0}
 
         def psum_bank(shape, dtype, ring="s"):
-            bank = psum.tile(shape, dtype, name="bank", tag="bank%d" % (len(banks_handed_out) % PSUM_BANKS))
-            banks_handed_out.append(bank)
+            first, n = rings[ring]
+            bank = psum.tile(shape, dtype, name="bank", tag="bank%d" % (first + handed[ring] % n))
+            handed[ring] += 1
             return bank
 
         zeros = keep.tile([P, BANK], BF16)
@@ -95,6 +97,8 @@ def tile_objectattention_pa_kernel(tc, q, k, v, w_up, gamma, beta, mean, var, ou
         mean_scaled = keep.tile([P, C_TILES], F32)
         bn_shift = keep.tile([P, C_TILES], F32)
         nc.gpsimd.memset(minus_half[:], -0.5)
+        minus_one = keep.tile([P, 2], F32)
+        nc.gpsimd.memset(minus_one[:], -1.0)
         v_grouped = keep.tile([P, M_PASSES, C, PACK], BF16, align_bytes=64)
         v_codes = keep.tile([P, M_PASSES, C], U32, align_bytes=64)
         v_scales = keep.tile([P, M_PASSES, C], U8, align_bytes=64)
@@ -115,6 +119,7 @@ def tile_objectattention_pa_kernel(tc, q, k, v, w_up, gamma, beta, mean, var, ou
         score_banks = {}
         e_rows = {}
         eT_banks = {}
+        vT_banks = {}
         inv_banks = {}
         ctx_banks = {}
         y_banks = {}
@@ -133,26 +138,33 @@ def tile_objectattention_pa_kernel(tc, q, k, v, w_up, gamma, beta, mean, var, ou
                 stop=(a == C_TILES - 1),
             )
 
-        def scores(j):
+        def scores(j, left_extra, right_extra):
             open_score_banks(j)
-            for h in range(2):
+            for h, extra in ((0, left_extra), (1, right_extra)):
                 for a in range(C_TILES):
                     score_matmul(j, h, a)
+                    for call in extra[a::C_TILES]:
+                        call()
 
         def bank_maximum(j, h):
+            if h == 0:
+                nc.vector.tensor_reduce(
+                    out=neg_max[:, j, 0:1], in_=score_banks[j][0][:], axis=AXIS.X, op=ALU.max, negate=True
+                )
+                return
             negated = ring.tile([P, BANK], BF16)
             nc.vector.tensor_scalar(
                 out=negated[:],
                 in0=score_banks[j][h][:],
                 scalar1=-1.0,
-                scalar2=None if h == 0 else neg_max[:, j, 0:1],
+                scalar2=neg_max[:, j, 0:1],
                 op0=ALU.mult,
                 op1=ALU.min,
                 accum_out=neg_max[:, j, h : h + 1],
             )
 
         def exponentials(j):
-            e_row = ring.tile([P, N], BF16)
+            e_row = ring.tile([P, N], BF16, name="e_row", bufs=6)
             for g in range(M_PASSES):
                 nc.scalar.activation(
                     out=e_row[:, g * BANK : (g + 1) * BANK],
@@ -165,25 +177,41 @@ def tile_objectattention_pa_kernel(tc, q, k, v, w_up, gamma, beta, mean, var, ou
             e_rows[j] = e_row
 
         def row_sums_of(j):
-            nc.vector.tensor_add(out=row_sums[:, j : j + 2], in0=e_sums[:, j : j + 2, 0], in1=e_sums[:, j : j + 2, 1])
+            nc.gpsimd.tensor_tensor(
+                out=row_sums[:, j : j + 2], in0=e_sums[:, j : j + 2, 0], in1=e_sums[:, j : j + 2, 1], op=ALU.add
+            )
 
         def inverse_sums(j):
-            nc.vector.reciprocal(out=inv_sum[:, j : j + 2], in_=row_sums[:, j : j + 2])
+            nc.gpsimd.tensor_tensor(
+                out=inv_sum[:, j : j + 2], in0=row_sums[:, j : j + 2], in1=minus_one[:], op=ALU.pow
+            )
 
-        def transpose_e(j):
+        def transposes_of_e(j):
             eT = psum_bank([P, M_PASSES * 2, P], F32, "t")
             words = e_rows[j][:].bitcast(F32)
-            for x in range(M_PASSES * 2):
-                nc.tensor.transpose(out=eT[:, x, :], in_=words[:, x * P : (x + 1) * P], identity=ident_f32[:])
             eT_banks[j] = eT
+            return [
+                (lambda x=x: nc.tensor.transpose(out=eT[:, x, :], in_=words[:, x * P : (x + 1) * P], identity=ident_f32[:]))
+                for x in range(M_PASSES * 2)
+            ]
+
+        def transpose_e(j):
+            for call in transposes_of_e(j):
+                call()
+
+        def transposes_of_inv(j):
+            inv_ps = psum_bank([P, 2, P], F32)
+            inv_banks[j] = inv_ps
+            return [
+                (lambda x=x: nc.tensor.transpose(
+                    out=inv_ps[:, x, :], in_=inv_sum[:, j + x : j + x + 1].to_broadcast([P, P]), identity=ident_f32[:]
+                ))
+                for x in range(2)
+            ]
 
         def transpose_inv(j):
-            inv_ps = psum_bank([P, 2, P], F32, "s")
-            for x in range(2):
-                nc.tensor.transpose(
-                    out=inv_ps[:, x, :], in_=inv_sum[:, j + x : j + x + 1].to_broadcast([P, P]), identity=ident_f32[:]
-                )
-            inv_banks[j] = inv_ps
+            for call in transposes_of_inv(j):
+                call()
 
         def copy_out_e(j):
             grouped = ring.tile([P, M_PASSES, P, PACK], BF16, name="e_grouped", align_bytes=64)
@@ -265,51 +293,63 @@ def tile_objectattention_pa_kernel(tc, q, k, v, w_up, gamma, beta, mean, var, ou
 
         def project_tile(j):
             cols = slice(j * P, (j + 1) * P)
-            y_ps = psum_bank([P, C_TILES, P], F32)
-            for i in range(C_TILES):
-                nc.tensor.matmul_mx(
-                    out=y_ps[:, i, :],
-                    lhsT=w_codes[:, i * P : (i + 1) * P].bitcast(FP8X4),
-                    lhsT_scale=w_scales[:, i * P : (i + 1) * P],
-                    rhs=ctx_codes[:, cols].bitcast(FP8X4),
-                    rhs_scale=ctx_scales[:, cols],
-                    start=True,
-                    stop=True,
-                )
-            y_banks[j] = y_ps
+            for half in range(2):
+                y_ps = psum_bank([P, 2, P], F32)
+                for x in range(2):
+                    i = 2 * half + x
+                    nc.tensor.matmul_mx(
+                        out=y_ps[:, x, :],
+                        lhsT=w_codes[:, i * P : (i + 1) * P].bitcast(FP8X4),
+                        lhsT_scale=w_scales[:, i * P : (i + 1) * P],
+                        rhs=ctx_codes[:, cols].bitcast(FP8X4),
+                        rhs_scale=ctx_scales[:, cols],
+                        start=True,
+                        stop=True,
+                    )
+                y_banks[j, half] = y_ps
 
-        def finish_tile(j):
+        def finish_tile_scalar(j, half):
             cols = slice(j * P, (j + 1) * P)
-            y_ps = y_banks[j]
-            for i in (0, 1):
+            for x in range(2):
+                i = 2 * half + x
                 nc.scalar.activation(
                     out=out_sb[:, i, cols],
-                    in_=y_ps[:, i, :],
+                    in_=y_banks[j, half][:, x, :],
                     func=ACT.Relu,
                     bias=bn_shift[:, i : i + 1],
                     scale=bn_scale[:, i : i + 1],
                 )
-            for i in (2, 3):
+            nc.sync.dma_start(out=out_view[:, 2 * half : 2 * half + 2, cols], in_=out_sb[:, 2 * half : 2 * half + 2, cols])
+
+        def finish_tile_vector(j, half):
+            cols = slice(j * P, (j + 1) * P)
+            both = slice(2 * half, 2 * half + 2)
+            for x in range(2):
+                i = 2 * half + x
                 nc.vector.tensor_scalar(
                     out=out_sb[:, i, cols],
-                    in0=y_ps[:, i, :],
+                    in0=y_banks[j, half][:, x, :],
                     scalar1=bn_scale[:, i : i + 1],
                     scalar2=bn_shift[:, i : i + 1],
                     op0=ALU.mult,
                     op1=ALU.add,
                 )
-            nc.vector.tensor_scalar_max(out=out_sb[:, 2:4, cols], in0=out_sb[:, 2:4, cols], scalar1=0.0)
-            for half in (slice(0, 2), slice(2, 4)):
-                nc.sync.dma_start(out=out_view[:, half, cols], in_=out_sb[:, half, cols])
+            nc.vector.tensor_scalar_max(out=out_sb[:, both, cols], in0=out_sb[:, both, cols], scalar1=0.0)
+            nc.sync.dma_start(out=out_view[:, both, cols], in_=out_sb[:, both, cols])
 
-        def transpose_v(t, copy):
+        def transposes_of_v(t):
             words = v_sb[:, t // 2, t % 2, :].bitcast(F32)
             vT = psum_bank([P, M_PASSES * 2, P], F32, "t")
-            for x in range(M_PASSES * 2):
-                nc.tensor.transpose(out=vT[:, x, :], in_=words[:, x * P : (x + 1) * P], identity=ident_f32[:])
+            vT_banks[t] = vT
+            return [
+                (lambda x=x: nc.tensor.transpose(out=vT[:, x, :], in_=words[:, x * P : (x + 1) * P], identity=ident_f32[:]))
+                for x in range(M_PASSES * 2)
+            ]
+
+        def copy_out_v(t, copy):
             copy(
                 out=v_grouped[:].bitcast(F32)[:, :, t * P : (t + 1) * P, :],
-                in_=vT[:].rearrange("p (g u) c -> p g c u", u=2),
+                in_=vT_banks[t][:].rearrange("p (g u) c -> p g c u", u=2),
             )
 
         def quantise_v(g):
@@ -345,8 +385,9 @@ def tile_objectattention_pa_kernel(tc, q, k, v, w_up, gamma, beta, mean, var, ou
             return 0 <= j < N_TILES
 
         T, C_, Q, E, X, Y, Z = transpose_e, copy_out_e, quantise_e, exponentials, context, divide, quantise_ctx
-        PT, LT = project_tile, finish_tile
+        PT, LS, LV = project_tile, finish_tile_scalar, finish_tile_vector
         R = row_sums_of
+        WT, WQ, VQ = transpose_w, quantise_w, quantise_v
         PR, L, I, B, D = project, finish, inverse_sums, transpose_inv, copy_out_inv
         batch_norm()
         open_score_banks(0)
@@ -360,40 +401,57 @@ def tile_objectattention_pa_kernel(tc, q, k, v, w_up, gamma, beta, mean, var, ou
         for j in range(2):
             bank_maximum(j, 0)
             bank_maximum(j, 1)
-            exponentials(j)
+        exponentials(0)
+        BETWEEN = {
+            3: [(R, (0,))],
+            5: [(VQ, (1,)), (R, (2,))],
+            6: [(WT, (0,))],
+            7: [(WQ, ()), (R, (4,))],
+        }
+        AFTER = {
+            3: [(I, (0,))],
+            4: [(VQ, (0,)), (Q, (0,))],
+            5: [(Q, (1,)), (I, (2,))],
+            6: [(Q, (2,)), (Q, (3,)), (WT, (1,)), (Z, (0,))],
+            7: [(I, (4,)), (Q, (4,)), (Z, (1,)), (Q, (5,))],
+        }
+        plan = {2: ((), (("V", 0),)), 3: ((("V", 1),), (("V", 2),)), 4: ((("V", 3),), (("T", 0),)), 5: ((("T", 1), ("B", 0)), (("T", 2),)), 6: ((("T", 3),), (("T", 4),)), 7: ((("B", 2),), (("T", 5),))}
+        of = {"V": transposes_of_v, "T": transposes_of_e, "B": transposes_of_inv}
+        on_vector = (1, 3)
         for s in range(2, N_TILES):
-            scores(s)
-            bank_maximum(s, 0)
-            if s in (4, 5):
-                quantise_v(s - 4)
-            else:
-                if s >= 6:
-                    transpose_w(s - 6)
-            if s in (4, 6):
-                row_sums_of(s - 4)
-            bank_maximum(s, 1)
-            if s in (4, 6):
-                inverse_sums(s - 4)
-            transpose_e(s - 2)
-            copy_out_e(s - 2)
-            if s < 4:
-                transpose_v(2 * s - 4, nc.vector.tensor_copy)
-            if s in (5, 7):
-                transpose_inv(s - 5)
-                copy_out_inv(s - 5)
+            open_score_banks(s)
+            for h in range(2):
+                calls = []
+                for kind, which in plan[s][h]:
+                    calls = calls + of[kind](which)
+                for a in range(C_TILES):
+                    score_matmul(s, h, a)
+                    for call in calls[a::C_TILES]:
+                        call()
+                if h == 1:
+                    for call, args in BETWEEN.get(s, ()):
+                        call(*args)
+                bank_maximum(s, h)
+                for kind, which in plan[s][h]:
+                    if kind == "T":
+                        copy_out_e(which)
+                    if kind == "B":
+                        copy_out_inv(which)
+                    if kind == "V":
+                        copy_out_v(which, nc.vector.tensor_copy if which in on_vector else nc.scalar.copy)
+            if s == 2:
+                exponentials(1)
             exponentials(s)
-            if s < 4:
-                transpose_v(2 * s - 3, nc.scalar.copy)
-            quantise_e(s - 2)
-            if s >= 6:
-                context(s - 6)
-                divide(s - 6)
-        quantise_ctx(0)
+            for call, args in AFTER.get(s, ()):
+                call(*args)
+            if s >= 5:
+                context(s - 5)
+                divide(s - 5)
         TAIL = [
-            [(R, (4,)), (T, (6,)), (C_, (6,)), (X, (2,)), (quantise_w, ()), (I, (4,)), (Z, (1,)), (Q, (6,)), (Y, (2,)), (X, (3,)), (Z, (2,)), (Y, (3,))],
-            [(B, (4,)), (T, (7,)), (D, (4,)), (C_, (7,)), (PR, (0, 0)), (PR, (0, 1)), (R, (6,)), (Z, (3,)), (I, (6,)), (L, (0, 0)), (X, (4,)), (Q, (7,)), (Y, (4,)), (L, (0, 1)), (X, (5,)), (B, (6,)), (D, (6,)), (Z, (4,)), (Y, (5,))],
-            [(PR, (1, 0)), (PR, (1, 1)), (L, (1, 0)), (L, (1, 1)), (X, (6,)), (Z, (5,)), (Y, (6,)), (X, (7,)), (Z, (6,)), (Y, (7,)), (PR, (2, 0)), (PR, (2, 1)), (L, (2, 0)), (L, (2, 1)), (PT, (6,)), (Z, (7,)), (LT, (6,))],
-            [(PT, (7,)), (LT, (7,))],
+            [(T, (6,)), (C_, (6,)), (X, (3,)), (Y, (3,)), (Z, (2,)), (R, (6,)), (Q, (6,)), (I, (6,))],
+            [(B, (4,)), (D, (4,)), (X, (4,)), (T, (7,)), (C_, (7,)), (Z, (3,)), (Y, (4,)), (PR, (0, 0)), (PR, (0, 1)), (L, (0, 0)), (L, (0, 1)), (X, (5,)), (Q, (7,)), (B, (6,)), (D, (6,)), (Z, (4,)), (Y, (5,))],
+            [(PR, (1, 0)), (PR, (1, 1)), (L, (1, 0)), (L, (1, 1)), (X, (6,)), (Z, (5,)), (Y, (6,)), (X, (7,)), (Z, (6,)), (Y, (7,)), (PR, (2, 0)), (PR, (2, 1)), (L, (2, 0)), (L, (2, 1)), (PT, (6,)), (Z, (7,)), (LS, (6, 0)), (LS, (6, 1))],
+            [(PT, (7,)), (LS, (7, 0)), (LV, (7, 1))],
         ]
         for step in TAIL:
             for call, args in step:

@@ -23,7 +23,7 @@ N_TILES = N // P
 M_PASSES = N // K_PASS
 PAIR = 2 * P
 PSUM_BANKS = 8
-WARM_UP = 4
+WARM_UP = 16
 EPS = 1e-5
 SB = 6
 
@@ -51,11 +51,11 @@ def tile_objectattention_pa_kernel(tc, q, k, v, w_up, gamma, beta, mean, var, ou
             handed[ring] += 1
             return bank
 
-        zeros = keep.tile([P, BANK], BF16)
+        zeros = keep.tile([P, P], BF16)
         nc.vector.memset(zeros[:], 0.0)
-        warm_ps = psum_bank([P, BANK], F32, "t")
+        warm_ps = psum_bank([P, P], F32, "t")
         for x in range(WARM_UP):
-            nc.tensor.matmul(out=warm_ps[:], lhsT=zeros[:, 0:P], rhs=zeros[:], start=True, stop=True)
+            nc.tensor.matmul(out=warm_ps[:], lhsT=zeros[:], rhs=zeros[:], start=True, stop=True)
 
         q_view = q[0].rearrange("(p a) h w -> p a (h w)", a=C_TILES)
         k_view = k[0].rearrange("(p a) h w -> p a (h w)", a=C_TILES)
@@ -186,8 +186,8 @@ def tile_objectattention_pa_kernel(tc, q, k, v, w_up, gamma, beta, mean, var, ou
                 out=inv_sum[:, j : j + 2], in0=row_sums[:, j : j + 2], in1=minus_one[:], op=ALU.pow
             )
 
-        def transposes_of_e(j):
-            eT = psum_bank([P, M_PASSES * 2, P], F32, "t")
+        def transposes_of_e(j, ring="t"):
+            eT = psum_bank([P, M_PASSES * 2, P], F32, ring)
             words = e_rows[j][:].bitcast(F32)
             eT_banks[j] = eT
             return [
@@ -195,8 +195,8 @@ def tile_objectattention_pa_kernel(tc, q, k, v, w_up, gamma, beta, mean, var, ou
                 for x in range(M_PASSES * 2)
             ]
 
-        def transpose_e(j):
-            for call in transposes_of_e(j):
+        def transpose_e(j, ring="t"):
+            for call in transposes_of_e(j, ring):
                 call()
 
         def transposes_of_inv(j):
@@ -228,8 +228,8 @@ def tile_objectattention_pa_kernel(tc, q, k, v, w_up, gamma, beta, mean, var, ou
                 in_=e_grouped[j][:].rearrange("p g n t -> p (g n t)"),
             )
 
-        def context(j):
-            ctx_ps = psum_bank([P, PACK, P], F32)
+        def context(j, ring="s"):
+            ctx_ps = psum_bank([P, PACK, P], F32, ring)
             for t in range(PACK):
                 for g in range(M_PASSES):
                     nc.tensor.matmul_mx(
@@ -261,9 +261,9 @@ def tile_objectattention_pa_kernel(tc, q, k, v, w_up, gamma, beta, mean, var, ou
                 in_=ctx_grouped[j][:].rearrange("p n t -> p (n t)"),
             )
 
-        def project(pair, half):
+        def project(pair, half, ring="s"):
             cols = slice(pair * PAIR, (pair + 1) * PAIR)
-            y_ps = psum_bank([P, 2, PAIR], F32)
+            y_ps = psum_bank([P, 2, PAIR], F32, ring)
             for x in range(2):
                 i = 2 * half + x
                 nc.tensor.matmul_mx(
@@ -405,17 +405,17 @@ def tile_objectattention_pa_kernel(tc, q, k, v, w_up, gamma, beta, mean, var, ou
         BETWEEN = {
             3: [(R, (0,))],
             5: [(VQ, (1,)), (R, (2,))],
-            6: [(WT, (0,))],
-            7: [(WQ, ()), (R, (4,))],
+            6: [(WT, (1,))],
+            7: [(R, (4,)), (Q, (4,)), (Z, (1,))],
         }
         AFTER = {
             3: [(I, (0,))],
             4: [(VQ, (0,)), (Q, (0,))],
             5: [(Q, (1,)), (I, (2,))],
-            6: [(Q, (2,)), (Q, (3,)), (WT, (1,)), (Z, (0,))],
-            7: [(I, (4,)), (Q, (4,)), (Z, (1,)), (Q, (5,))],
+            6: [(Q, (2,)), (Q, (3,)), (Z, (0,)), (WQ, ())],
+            7: [(I, (4,)), (Q, (5,))],
         }
-        plan = {2: ((), (("V", 0),)), 3: ((("V", 1),), (("V", 2),)), 4: ((("V", 3),), (("T", 0),)), 5: ((("T", 1), ("B", 0)), (("T", 2),)), 6: ((("T", 3),), (("T", 4),)), 7: ((("B", 2),), (("T", 5),))}
+        plan = {2: ((), (("V", 0),)), 3: ((("V", 1),), (("V", 2),)), 4: ((("V", 3),), (("T", 0),)), 5: ((("T", 1), ("B", 0)), (("T", 2),)), 6: ((("T", 3),), (("T", 4),)), 7: ((("T", 5), ("B", 2)), (("T", 6),))}
         of = {"V": transposes_of_v, "T": transposes_of_e, "B": transposes_of_inv}
         on_vector = (1, 3)
         for s in range(2, N_TILES):
@@ -447,10 +447,12 @@ def tile_objectattention_pa_kernel(tc, q, k, v, w_up, gamma, beta, mean, var, ou
             if s >= 5:
                 context(s - 5)
                 divide(s - 5)
+            if s == 5:
+                transpose_w(0)
         TAIL = [
-            [(T, (6,)), (C_, (6,)), (X, (3,)), (Y, (3,)), (Z, (2,)), (R, (6,)), (Q, (6,)), (I, (6,))],
-            [(B, (4,)), (D, (4,)), (X, (4,)), (T, (7,)), (C_, (7,)), (Z, (3,)), (Y, (4,)), (PR, (0, 0)), (PR, (0, 1)), (L, (0, 0)), (L, (0, 1)), (X, (5,)), (Q, (7,)), (B, (6,)), (D, (6,)), (Z, (4,)), (Y, (5,))],
-            [(PR, (1, 0)), (PR, (1, 1)), (L, (1, 0)), (L, (1, 1)), (X, (6,)), (Z, (5,)), (Y, (6,)), (X, (7,)), (Z, (6,)), (Y, (7,)), (PR, (2, 0)), (PR, (2, 1)), (L, (2, 0)), (L, (2, 1)), (PT, (6,)), (Z, (7,)), (LS, (6, 0)), (LS, (6, 1))],
+            [(X, (3,)), (Q, (6,)), (Y, (3,)), (Z, (2,)), (PR, (0, 0, "t")), (PR, (0, 1, "t")), (B, (4,)), (R, (6,)), (I, (6,)), (D, (4,)), (L, (0, 0))],
+            [(X, (4,)), (T, (7, "s")), (C_, (7,)), (L, (0, 1)), (Z, (3,)), (Y, (4,)), (X, (5,)), (Q, (7,)), (B, (6,)), (D, (6,)), (Z, (4,)), (Y, (5,)), (X, (6,)), (Z, (5,)), (Y, (6,))],
+            [(PR, (1, 0)), (PR, (1, 1)), (L, (1, 0)), (L, (1, 1)), (X, (7,)), (Z, (6,)), (Y, (7,)), (PR, (2, 0)), (PR, (2, 1)), (L, (2, 0)), (L, (2, 1)), (PT, (6,)), (Z, (7,)), (LS, (6, 0)), (LS, (6, 1))],
             [(PT, (7,)), (LS, (7, 0)), (LV, (7, 1))],
         ]
         for step in TAIL:

from contextlib import ExitStack

import concourse.mybir as mybir
from concourse.masks import make_identity

F32 = mybir.dt.float32
BF16 = mybir.dt.bfloat16
U32 = mybir.dt.uint32
U8 = mybir.dt.uint8
FP8X4 = mybir.dt.float8_e4m3fn_x4
ALU = mybir.AluOpType
ACT = mybir.ActivationFunctionType
AXIS = mybir.AxisListType

P = 128
C = 512
N = 1024
PACK = 4
K_PASS = P * PACK
BANK = 512
C_TILES = C // P
N_TILES = N // P
M_PASSES = N // K_PASS
PAIR = 2 * P
PSUM_BANKS = 8
WARM_UP = 16
EPS = 1e-5
SB = 6

LAG_T = 2
LAG_X = 5
LAG_Y = 8

FLOPS = 2 * N * N * C * 2 + 2 * C * C * N


def tile_objectattention_pa_kernel(tc, q, k, v, w_up, gamma, beta, mean, var, out):
    nc = tc.nc
    with ExitStack() as ctx:
        ctx.enter_context(tc.manual_schedule())
        keep = ctx.enter_context(tc.tile_pool(name="keep", bufs=1))
        ring = ctx.enter_context(tc.tile_pool(name="ring", bufs=3))
        psum = ctx.enter_context(tc.psum_pool(name="psum", bufs=1))

        rings = {"s": (0, SB), "t": (SB, PSUM_BANKS - SB)}
        handed = {"s": 0, "t": 0}

        def psum_bank(shape, dtype, ring="s"):
            first, n = rings[ring]
            bank = psum.tile(shape, dtype, name="bank", tag="bank%d" % (first + handed[ring] % n))
            handed[ring] += 1
            return bank

        zeros = keep.tile([P, P], BF16)
        nc.vector.memset(zeros[:], 0.0)
        warm_ps = psum_bank([P, P], F32, "t")
        for x in range(WARM_UP):
            nc.tensor.matmul(out=warm_ps[:], lhsT=zeros[:], rhs=zeros[:], start=True, stop=True)

        q_view = q[0].rearrange("(p a) h w -> p a (h w)", a=C_TILES)
        k_view = k[0].rearrange("(p a) h w -> p a (h w)", a=C_TILES)
        q_sb = keep.tile([P, C_TILES, N], BF16)
        k_sb = keep.tile([P, C_TILES, N], BF16)
        left, right = slice(0, BANK), slice(BANK, N)
        nc.sync.dma_start(out=q_sb[:, 0, 0:PAIR], in_=q_view[:, 0, 0:PAIR])
        nc.sync.dma_start(out=k_sb[:, 0, left], in_=k_view[:, 0, left])
        nc.sync.dma_start(out=k_sb[:, 0, right], in_=k_view[:, 0, right])
        for a in range(1, C_TILES):
            nc.sync.dma_start(out=q_sb[:, a, 0:PAIR], in_=q_view[:, a, 0:PAIR])
            nc.sync.dma_start(out=k_sb[:, a, :], in_=k_view[:, a, :])
        nc.sync.dma_start(out=q_sb[:, :, PAIR:N], in_=q_view[:, :, PAIR:N])
        v_view = v[0].rearrange("(u p b) h w -> p u b (h w)", u=2, b=2)
        v_sb = keep.tile([P, 2, 2, N], BF16)
        for u in range(2):
            nc.sync.dma_start(out=v_sb[:, u, :, :], in_=v_view[:, u, :, :])
        gamma_sb = keep.tile([P, C_TILES], BF16)
        beta_sb = keep.tile([P, C_TILES], BF16)
        mean_sb = keep.tile([P, C_TILES], BF16)
        var_sb = keep.tile([P, C_TILES], BF16)
        nc.sync.dma_start(out=var_sb[:], in_=var.rearrange("(i p) -> p i", i=C_TILES))
        nc.sync.dma_start(out=gamma_sb[:], in_=gamma.rearrange("(i p) -> p i", i=C_TILES))
        nc.sync.dma_start(out=mean_sb[:], in_=mean.rearrange("(i p) -> p i", i=C_TILES))
        nc.sync.dma_start(out=beta_sb[:], in_=beta.rearrange("(i p) -> p i", i=C_TILES))
        w_raw = keep.tile([P, C // 16, 64], BF16, align_bytes=64)
        w_view = w_up.rearrange("(y j) (u a k) -> u a j y k", j=16, u=2, a=4)
        for u in range(2):
            for a in range(4):
                nc.sync.dma_start(out=w_raw[32 * a + u : 32 * a + 32 : 2, :, :], in_=w_view[u, a])
        out_view = out[0].rearrange("(i p) h w -> p i (h w)", i=C_TILES)
        ident_f32 = keep.tile([P, P], F32)
        make_identity(nc, ident_f32[:])

        var_eps = keep.tile([P, C_TILES], F32)
        minus_half = keep.tile([P, C_TILES], F32)
        inv_std = keep.tile([P, C_TILES], F32)
        bn_scale = keep.tile([P, C_TILES], F32)
        mean_scaled = keep.tile([P, C_TILES], F32)
        bn_shift = keep.tile([P, C_TILES], F32)
        nc.gpsimd.memset(minus_half[:], -0.5)
        minus_one = keep.tile([P, 2], F32)
        nc.gpsimd.memset(minus_one[:], -1.0)
        v_grouped = keep.tile([P, M_PASSES, C, PACK], BF16, align_bytes=64)
        v_codes = keep.tile([P, M_PASSES, C], U32, align_bytes=64)
        v_scales = keep.tile([P, M_PASSES, C], U8, align_bytes=64)
        w_grouped = keep.tile([P, C, PACK], BF16, align_bytes=64)
        w_codes = keep.tile([P, C], U32, align_bytes=64)
        w_scales = keep.tile([P, C], U8, align_bytes=64)
        e_codes = keep.tile([P, N_TILES, M_PASSES, P], U32, align_bytes=64)
        e_scales = keep.tile([P, N_TILES, M_PASSES, P], U8, align_bytes=64)
        inv_sum_bcast = keep.tile([P, N_TILES, P], F32)
        ctx_codes = keep.tile([P, N], U32, align_bytes=64)
        ctx_scales = keep.tile([P, N], U8, align_bytes=64)
        out_sb = keep.tile([P, C_TILES, N], F32)
        neg_max = keep.tile([P, N_TILES, M_PASSES], F32)
        e_sums = keep.tile([P, N_TILES, M_PASSES], F32)
        row_sums = keep.tile([P, N_TILES], F32)
        inv_sum = keep.tile([P, N_TILES], F32)

        score_banks = {}
        e_rows = {}
        eT_banks = {}
        vT_banks = {}
        inv_banks = {}
        ctx_banks = {}
        y_banks = {}
        e_grouped = {}
        ctx_grouped = {}

        def open_score_banks(j):
            score_banks[j] = [psum_bank([P, BANK], F32) for h in range(2)]

        def score_matmul(j, h, a):
            nc.tensor.matmul(
                out=score_banks[j][h][:],
                lhsT=q_sb[:, a, j * P : (j + 1) * P],
                rhs=k_sb[:, a, h * BANK : (h + 1) * BANK],
                start=(a == 0),
                stop=(a == C_TILES - 1),
            )

        def scores(j, left_extra, right_extra):
            open_score_banks(j)
            for h, extra in ((0, left_extra), (1, right_extra)):
                for a in range(C_TILES):
                    score_matmul(j, h, a)
                    for call in extra[a::C_TILES]:
                        call()

        def bank_maximum(j, h):
            if h == 0:
                nc.vector.tensor_reduce(
                    out=neg_max[:, j, 0:1], in_=score_banks[j][0][:], axis=AXIS.X, op=ALU.max, negate=True
                )
                return
            negated = ring.tile([P, BANK], BF16)
            nc.vector.tensor_scalar(
                out=negated[:],
                in0=score_banks[j][h][:],
                scalar1=-1.0,
                scalar2=neg_max[:, j, 0:1],
                op0=ALU.mult,
                op1=ALU.min,
                accum_out=neg_max[:, j, h : h + 1],
            )

        def exponentials(j):
            e_row = ring.tile([P, N], BF16, name="e_row", bufs=6)
            for g in range(M_PASSES):
                nc.scalar.activation(
                    out=e_row[:, g * BANK : (g + 1) * BANK],
                    in_=score_banks[j][g][:],
                    func=ACT.Exp,
                    bias=neg_max[:, j, 1:2],
                    scale=1.0,
                    accum_out=e_sums[:, j, g : g + 1],
                )
            e_rows[j] = e_row

        def row_sums_of(j):
            nc.gpsimd.tensor_tensor(
                out=row_sums[:, j : j + 2], in0=e_sums[:, j : j + 2, 0], in1=e_sums[:, j : j + 2, 1], op=ALU.add
            )

        def inverse_sums(j):
            nc.gpsimd.tensor_tensor(
                out=inv_sum[:, j : j + 2], in0=row_sums[:, j : j + 2], in1=minus_one[:], op=ALU.pow
            )

        def transposes_of_e(j, ring="t"):
            eT = psum_bank([P, M_PASSES * 2, P], F32, ring)
            words = e_rows[j][:].bitcast(F32)
            eT_banks[j] = eT
            return [
                (lambda x=x: nc.tensor.transpose(out=eT[:, x, :], in_=words[:, x * P : (x + 1) * P], identity=ident_f32[:]))
                for x in range(M_PASSES * 2)
            ]

        def transpose_e(j, ring="t"):
            for call in transposes_of_e(j, ring):
                call()

        def transposes_of_inv(j):
            inv_ps = psum_bank([P, 2, P], F32)
            inv_banks[j] = inv_ps
            return [
                (lambda x=x: nc.tensor.transpose(
                    out=inv_ps[:, x, :], in_=inv_sum[:, j + x : j + x + 1].to_broadcast([P, P]), identity=ident_f32[:]
                ))
                for x in range(2)
            ]

        def transpose_inv(j):
            for call in transposes_of_inv(j):
                call()

        def copy_out_e(j):
            grouped = ring.tile([P, M_PASSES, P, PACK], BF16, name="e_grouped", align_bytes=64)
            nc.scalar.copy(out=grouped[:].bitcast(F32), in_=eT_banks[j][:].rearrange("p (g u) n -> p g n u", u=2))
            e_grouped[j] = grouped

        def copy_out_inv(j):
            nc.scalar.copy(out=inv_sum_bcast[:, j : j + 2, :], in_=inv_banks[j][:])

        def quantise_e(j):
            nc.vector.quantize_mx(
                out=e_codes[:, j, :, :].rearrange("p g n -> p (g n)").bitcast(FP8X4),
                scales=e_scales[:, j, :, :].rearrange("p g n -> p (g n)"),
                in_=e_grouped[j][:].rearrange("p g n t -> p (g n t)"),
            )

        def context(j, ring="s"):
            ctx_ps = psum_bank([P, PACK, P], F32, ring)
            for t in range(PACK):
                for g in range(M_PASSES):
                    nc.tensor.matmul_mx(
                        out=ctx_ps[:, t, :],
                        lhsT=v_codes[:, g, t * P : (t + 1) * P].bitcast(FP8X4),
                        lhsT_scale=v_scales[:, g, t * P : (t + 1) * P],
                        rhs=e_codes[:, j, g, :].bitcast(FP8X4),
                        rhs_scale=e_scales[:, j, g, :],
                        start=(g == 0),
                        stop=(g == M_PASSES - 1),
                    )
            ctx_banks[j] = ctx_ps

        def divide(j):
            ctx_ps = ctx_banks[j]
            grouped = ring.tile([P, P, PACK], BF16, name="ctx_grouped", align_bytes=64)
            nc.vector.tensor_tensor(
                out=grouped[:],
                in0=ctx_ps[:].rearrange("p t n -> p n t"),
                in1=inv_sum_bcast[:, j, :].unsqueeze(2).to_broadcast([P, P, PACK]),
                op=ALU.mult,
            )
            ctx_grouped[j] = grouped

        def quantise_ctx(j):
            nc.vector.quantize_mx(
                out=ctx_codes[:, j * P : (j + 1) * P].bitcast(FP8X4),
                scales=ctx_scales[:, j * P : (j + 1) * P],
                in_=ctx_grouped[j][:].rearrange("p n t -> p (n t)"),
            )

        def project(pair, half, ring="s"):
            cols = slice(pair * PAIR, (pair + 1) * PAIR)
            y_ps = psum_bank([P, 2, PAIR], F32, ring)
            for x in range(2):
                i = 2 * half + x
                nc.tensor.matmul_mx(
                    out=y_ps[:, x, :],
                    lhsT=w_codes[:, i * P : (i + 1) * P].bitcast(FP8X4),
                    lhsT_scale=w_scales[:, i * P : (i + 1) * P],
                    rhs=ctx_codes[:, cols].bitcast(FP8X4),
                    rhs_scale=ctx_scales[:, cols],
                    start=True,
                    stop=True,
                )
            y_banks[pair, half] = y_ps

        def finish(pair, half):
            cols = slice(pair * PAIR, (pair + 1) * PAIR)
            y_ps = y_banks[pair, half]
            for x in range(2):
                i = 2 * half + x
                nc.scalar.activation(
                    out=out_sb[:, i, cols],
                    in_=y_ps[:, x, :],
                    func=ACT.Relu,
                    bias=bn_shift[:, i : i + 1],
                    scale=bn_scale[:, i : i + 1],
                )
                nc.sync.dma_start(out=out_view[:, i, cols], in_=out_sb[:, i, cols])

        def project_tile(j):
            cols = slice(j * P, (j + 1) * P)
            for half in range(2):
                y_ps = psum_bank([P, 2, P], F32)
                for x in range(2):
                    i = 2 * half + x
                    nc.tensor.matmul_mx(
                        out=y_ps[:, x, :],
                        lhsT=w_codes[:, i * P : (i + 1) * P].bitcast(FP8X4),
                        lhsT_scale=w_scales[:, i * P : (i + 1) * P],
                        rhs=ctx_codes[:, cols].bitcast(FP8X4),
                        rhs_scale=ctx_scales[:, cols],
                        start=True,
                        stop=True,
                    )
                y_banks[j, half] = y_ps

        def finish_tile_scalar(j, half):
            cols = slice(j * P, (j + 1) * P)
            for x in range(2):
                i = 2 * half + x
                nc.scalar.activation(
                    out=out_sb[:, i, cols],
                    in_=y_banks[j, half][:, x, :],
                    func=ACT.Relu,
                    bias=bn_shift[:, i : i + 1],
                    scale=bn_scale[:, i : i + 1],
                )
            nc.sync.dma_start(out=out_view[:, 2 * half : 2 * half + 2, cols], in_=out_sb[:, 2 * half : 2 * half + 2, cols])

        def finish_tile_vector(j, half):
            cols = slice(j * P, (j + 1) * P)
            both = slice(2 * half, 2 * half + 2)
            for x in range(2):
                i = 2 * half + x
                nc.vector.tensor_scalar(
                    out=out_sb[:, i, cols],
                    in0=y_banks[j, half][:, x, :],
                    scalar1=bn_scale[:, i : i + 1],
                    scalar2=bn_shift[:, i : i + 1],
                    op0=ALU.mult,
                    op1=ALU.add,
                )
            nc.vector.tensor_scalar_max(out=out_sb[:, both, cols], in0=out_sb[:, both, cols], scalar1=0.0)
            nc.sync.dma_start(out=out_view[:, both, cols], in_=out_sb[:, both, cols])

        def transposes_of_v(t):
            words = v_sb[:, t // 2, t % 2, :].bitcast(F32)
            vT = psum_bank([P, M_PASSES * 2, P], F32, "t")
            vT_banks[t] = vT
            return [
                (lambda x=x: nc.tensor.transpose(out=vT[:, x, :], in_=words[:, x * P : (x + 1) * P], identity=ident_f32[:]))
                for x in range(M_PASSES * 2)
            ]

        def copy_out_v(t, copy):
            copy(
                out=v_grouped[:].bitcast(F32)[:, :, t * P : (t + 1) * P, :],
                in_=vT_banks[t][:].rearrange("p (g u) c -> p g c u", u=2),
            )

        def quantise_v(g):
            nc.vector.quantize_mx(
                out=v_codes[:, g, :].bitcast(FP8X4),
                scales=v_scales[:, g, :],
                in_=v_grouped[:, g, :, :].rearrange("p c t -> p (c t)"),
            )

        def transpose_w(half):
            rows = slice(half * C // 2, (half + 1) * C // 2)
            blocks = slice(half * C // 32, (half + 1) * C // 32)
            nc.vector.transpose(
                out=w_grouped[:, rows, :].rearrange("p o t -> p (o t)").bitcast(F32),
                in_=w_raw[:, blocks, :].rearrange("p y k -> p (y k)").bitcast(F32),
            )

        def quantise_w():
            nc.vector.quantize_mx(
                out=w_codes[:].bitcast(FP8X4),
                scales=w_scales[:],
                in_=w_grouped[:].rearrange("p o t -> p (o t)"),
            )

        def batch_norm():
            nc.gpsimd.tensor_scalar_add(out=var_eps[:], in0=var_sb[:], scalar1=EPS)
            nc.gpsimd.tensor_tensor(out=inv_std[:], in0=var_eps[:], in1=minus_half[:], op=ALU.pow)
            nc.gpsimd.tensor_mul(out=bn_scale[:], in0=gamma_sb[:], in1=inv_std[:])
            nc.gpsimd.tensor_mul(out=mean_scaled[:], in0=mean_sb[:], in1=bn_scale[:])
            nc.gpsimd.tensor_sub(out=bn_shift[:], in0=beta_sb[:], in1=mean_scaled[:])

        def is_tile(j):
            return 0 <= j < N_TILES

        T, C_, Q, E, X, Y, Z = transpose_e, copy_out_e, quantise_e, exponentials, context, divide, quantise_ctx
        PT, LS, LV = project_tile, finish_tile_scalar, finish_tile_vector
        R = row_sums_of
        WT, WQ, VQ = transpose_w, quantise_w, quantise_v
        PR, L, I, B, D = project, finish, inverse_sums, transpose_inv, copy_out_inv
        batch_norm()
        open_score_banks(0)
        open_score_banks(1)
        for a in range(C_TILES):
            for h in range(2):
                for j in range(2):
                    score_matmul(j, h, a)

        vcopy = nc.vector.tensor_copy
        for j in range(2):
            bank_maximum(j, 0)
            bank_maximum(j, 1)
        exponentials(0)
        BETWEEN = {
            3: [(R, (0,))],
            5: [(VQ, (1,)), (R, (2,))],
            6: [(WT, (1,))],
            7: [(R, (4,)), (Q, (4,)), (Z, (1,))],
        }
        AFTER = {
            3: [(I, (0,))],
            4: [(VQ, (0,)), (Q, (0,))],
            5: [(Q, (1,)), (I, (2,))],
            6: [(Q, (2,)), (Q, (3,)), (Z, (0,)), (WQ, ())],
            7: [(I, (4,)), (Q, (5,))],
        }
        plan = {2: ((), (("V", 0),)), 3: ((("V", 1),), (("V", 2),)), 4: ((("V", 3),), (("T", 0),)), 5: ((("T", 1), ("B", 0)), (("T", 2),)), 6: ((("T", 3),), (("T", 4),)), 7: ((("T", 5), ("B", 2)), (("T", 6),))}
        of = {"V": transposes_of_v, "T": transposes_of_e, "B": transposes_of_inv}
        on_vector = (1, 3)
        for s in range(2, N_TILES):
            open_score_banks(s)
            for h in range(2):
                calls = []
                for kind, which in plan[s][h]:
                    calls = calls + of[kind](which)
                for a in range(C_TILES):
                    score_matmul(s, h, a)
                    for call in calls[a::C_TILES]:
                        call()
                if h == 1:
                    for call, args in BETWEEN.get(s, ()):
                        call(*args)
                bank_maximum(s, h)
                for kind, which in plan[s][h]:
                    if kind == "T":
                        copy_out_e(which)
                    if kind == "B":
                        copy_out_inv(which)
                    if kind == "V":
                        copy_out_v(which, nc.vector.tensor_copy if which in on_vector else nc.scalar.copy)
            if s == 2:
                exponentials(1)
            exponentials(s)
            for call, args in AFTER.get(s, ()):
                call(*args)
            if s >= 5:
                context(s - 5)
                divide(s - 5)
            if s == 5:
                transpose_w(0)
        TAIL = [
            [(X, (3,)), (Q, (6,)), (Y, (3,)), (Z, (2,)), (PR, (0, 0, "t")), (PR, (0, 1, "t")), (B, (4,)), (R, (6,)), (I, (6,)), (D, (4,)), (L, (0, 0))],
            [(X, (4,)), (T, (7, "s")), (C_, (7,)), (L, (0, 1)), (Z, (3,)), (Y, (4,)), (X, (5,)), (Q, (7,)), (B, (6,)), (D, (6,)), (Z, (4,)), (Y, (5,)), (X, (6,)), (Z, (5,)), (Y, (6,))],
            [(PR, (1, 0)), (PR, (1, 1)), (L, (1, 0)), (L, (1, 1)), (X, (7,)), (Z, (6,)), (Y, (7,)), (PR, (2, 0)), (PR, (2, 1)), (L, (2, 0)), (L, (2, 1)), (PT, (6,)), (Z, (7,)), (LS, (6, 0)), (LS, (6, 1))],
            [(PT, (7,)), (LS, (7, 0)), (LV, (7, 1))],
        ]
        for step in TAIL:
            for call, args in step:
                call(*args)
